import numpy as np
import ml_dtypes


def mxq(x, axis, fmt="e4m3"):
    dtype, down = {"e4m3": (ml_dtypes.float8_e4m3fn, 7), "e5m2": (ml_dtypes.float8_e5m2, 14)}[fmt]
    v = np.moveaxis(np.asarray(x, np.float32).astype(ml_dtypes.bfloat16).astype(np.float64), axis, -1)
    blocks = v.reshape(v.shape[:-1] + (-1, 32))
    amax = np.abs(blocks).max(-1, keepdims=True)
    byte = np.maximum(np.where(amax > 0, np.frexp(amax)[1] - 1 + 127, 0) - down, 1)
    scale = np.exp2(byte - 127.0)
    codes = (blocks / scale).astype(np.float32).astype(dtype).astype(np.float64)
    return np.moveaxis((codes * scale).reshape(v.shape), -1, axis)


WIDE = False


def mx_kscale(k):
    if not WIDE:
        return np.ones(k)
    levels = np.array([10, -10, 5, -5, 0])
    if k % 512:
        return np.exp2(np.random.permutation(np.resize(levels, k // 32))).repeat(32)
    a = np.empty((k // 512, 16))
    for p in range(k // 512):
        a[p, :8] = np.random.permutation(np.resize(levels, 8))
        for g in range(8):
            far = levels[np.abs(levels - a[p, g]) >= 10]
            a[p, g + 8] = far[np.random.randint(len(far))]
    return np.exp2(a.ravel()).repeat(32)


BF16 = ml_dtypes.bfloat16


def bf(x):
    return np.asarray(x, np.float32).astype(BF16)


def f64(x):
    return np.asarray(x).astype(np.float64)


B, L, H, HS, DV, C = 1, 1024, 1024, 1024, 1024, 512
SCALE_BASE = 2.0 ** 9


def xpos(x, downscale=False):
    n, d = x.shape[1], x.shape[-1]
    half = d // 2
    scale_vec = (np.arange(0, d, 2) + 0.4 * d) / (1.4 * d)
    pos = f64(np.arange(n))
    scale = scale_vec[None, :] ** (pos[:, None] / SCALE_BASE)
    if downscale:
        scale = 1.0 / scale
    inv_freq = 1.0 / (10000.0 ** (np.arange(half) / half))
    sinusoid = pos[:, None] * inv_freq[None, :]
    sin_s = np.repeat(np.sin(sinusoid) * scale, 2, axis=-1)
    cos_s = np.repeat(np.cos(sinusoid) * scale, 2, axis=-1)
    x1, x2 = x[..., ::2], x[..., 1::2]
    rot = np.stack((-x2, x1), axis=-1).reshape(x.shape)
    return x * cos_s + rot * sin_s


def draw0():
    s = mx_kscale(H)
    return {"X": bf(np.random.standard_normal((B, L, H)) * s),
            "W_Q": bf(np.random.standard_normal((H, HS)) * 0.4 / np.sqrt(H) / s[:, None]),
            "W_K": bf(np.random.standard_normal((H, HS)) * 0.4 / np.sqrt(H) / s[:, None])}


def core(X, W_Q, W_K):
    xq = mxq(f64(X), 2, "e4m3")
    Q = xpos(xq @ mxq(f64(W_Q), 0, "e4m3"))
    K = xpos(xq @ mxq(f64(W_K), 0, "e4m3"), downscale=True)
    return Q, K


def e4m3fn_bytes(y):
    return np.clip(np.asarray(y, np.float64), -448.0, 448.0).astype(np.float32).astype(ml_dtypes.float8_e4m3fn).view(np.uint8)


def e4m3fn_values(b):
    return np.asarray(b, np.uint8).view(ml_dtypes.float8_e4m3fn).astype(np.float64)


def setup_inputs():
    d = draw0()
    x0 = np.asarray(d['X']).astype(np.float64)
    s = (np.max(np.abs(x0), axis=(0, 1), keepdims=True) / 448.0).astype(np.float32)
    out = {}
    for k, v in d.items():
        if k == 'X':
            out['X_bytes'] = e4m3fn_bytes(x0 / s.astype(np.float64))
            out['X_scale'] = s
        else:
            out[k] = v
    return out


def reference(X_bytes, X_scale, W_Q, W_K):
    return core(e4m3fn_values(X_bytes) * X_scale.astype(np.float64), W_Q, W_K)

@@ -1,0 +1,346 @@
+from contextlib import ExitStack
+import math
+
+import concourse.mybir as mybir
+from concourse.masks import make_identity
+
+F32 = mybir.dt.float32
+BF16 = mybir.dt.bfloat16
+U8 = mybir.dt.uint8
+U32 = mybir.dt.uint32
+I32 = mybir.dt.int32
+FP8 = mybir.dt.float8_e4m3fn
+FP8X4 = mybir.dt.float8_e4m3fn_x4
+ALU = mybir.AluOpType
+ACT = mybir.ActivationFunctionType
+
+P = 128
+TOK = 1024
+KDIM = 1024
+CH = 1024
+FLOPS = 2 * TOK * KDIM * 2 * CH
+
+TWO_PI = 2.0 * math.pi
+WIL_ON_V = ((0, 0, 0), (0, 0, 1))
+
+
+def tile_simpleretention_pa_kernel(tc, X_bytes, X_scale, W_Q, W_K, out_0, out_1):
+    nc = tc.nc
+    weights = (W_Q, W_K)
+    outs = (
+        out_0.rearrange("b (t p) c -> p (b t) c", p=P),
+        out_1.rearrange("b (t p) c -> p (b t) c", p=P),
+    )
+    xb_view = X_bytes.rearrange("b (a p) k -> p (b a) k", p=P)
+
+    with ExitStack() as ctx:
+        const = ctx.enter_context(tc.tile_pool(name="const", bufs=1))
+        work = ctx.enter_context(tc.tile_pool(name="work", bufs=2))
+        ps_p = ctx.enter_context(tc.psum_pool(name="psp", bufs=2))
+        ps_o = ctx.enter_context(tc.psum_pool(name="pso", bufs=4))
+        ctx.enter_context(tc.manual_schedule(engines={mybir.EngineType.PE}))
+
+        xs = const.tile([P, KDIM], F32, name="xs")
+        nc.scalar.dma_start(out=xs[:], in_=X_scale.rearrange("a b k -> (a b k)").partition_broadcast(P))
+        xbytes = [const.tile([P, 4, KDIM], U8, name="xbytes%d" % h) for h in range(2)]
+        wraw = {}
+
+        def load_x(h):
+            nc.sync.dma_start(out=xbytes[h][:], in_=xb_view[:, 4 * h : 4 * h + 4, :])
+
+        def load_w(o, c):
+            for g in range(2):
+                t = work.tile([P, 4, 512], BF16, name="wraw", tag="wraw", bufs=6)
+                wraw[(o, c, g)] = t
+                nc.sync.dma_start(
+                    out=t[:],
+                    in_=weights[o][512 * g : 512 * (g + 1), 512 * c : 512 * (c + 1)].rearrange(
+                        "(p t) n -> p t n", t=4
+                    ),
+                )
+
+        load_x(0)
+        load_w(0, 0)
+        load_x(1)
+        load_w(0, 1)
+        load_w(1, 0)
+
+        ones = const.tile([P, 16], F32, name="ones")
+        nc.vector.memset(ones[:], 1.0)
+        ident = const.tile([P, P], F32, name="ident")
+        make_identity(nc, ident[:])
+        jcol = const.tile([P, 4], F32, name="jcol")
+        nc.gpsimd.iota(jcol[:], pattern=[[P, 4]], base=0, channel_multiplier=1, allow_small_or_imprecise_dtypes=True)
+        niota = const.tile([P, TOK], F32, name="niota")
+        nc.gpsimd.iota(niota[:], pattern=[[1, TOK]], base=0, channel_multiplier=0, allow_small_or_imprecise_dtypes=True)
+
+        zcol = const.tile([P, 4], F32, name="zcol")
+        nc.vector.tensor_scalar(
+            out=zcol[:], in0=jcol[:], scalar1=2.0 / (1.4 * 1024), scalar2=(0.4 * 1024) / (1.4 * 1024), op0=ALU.mult, op1=ALU.add
+        )
+        lnz = const.tile([P, 4], F32, name="lnz")
+        nc.scalar.activation(out=lnz[:], in_=zcol[:], func=ACT.Ln)
+        lsc = const.tile([P, 8], F32, name="lsc")
+        nc.vector.tensor_scalar(out=lsc[:, 0:4], in0=lnz[:], scalar1=1.0 / 512.0, scalar2=None, op0=ALU.mult)
+        nc.vector.tensor_scalar(out=lsc[:, 4:8], in0=lnz[:], scalar1=-1.0 / 512.0, scalar2=None, op0=ALU.mult)
+
+        vv = const.tile([P, 16], F32, name="vv")
+        for b in range(16):
+            nc.vector.tensor_scalar(
+                out=vv[:, b : b + 1], in0=ones[:, b : b + 1], scalar1=10000.0 ** (-b / 512.0), scalar2=None, op0=ALU.mult
+            )
+        rrow = const.tile([P, P], F32, name="rrow")
+        for a in range(8):
+            nc.vector.tensor_scalar(
+                out=rrow[:, 16 * a : 16 * a + 16],
+                in0=vv[:],
+                scalar1=10000.0 ** (-16.0 * a / 512.0) / TWO_PI,
+                scalar2=None,
+                op0=ALU.mult,
+            )
+        rt = ps_o.tile([P, 512], F32, name="rt", tag="ot")
+        nc.tensor.transpose(rt[:, 0:P], rrow[:], ident[:])
+        fcol = const.tile([P, 4], F32, name="fcol")
+        nc.vector.tensor_copy(out=fcol[:, 0:1], in_=rt[:, 0:1])
+        halfpi = const.tile([P, 1], F32, name="halfpi")
+        nc.vector.tensor_scalar(out=halfpi[:], in0=ones[:, 0:1], scalar1=0.5 * math.pi, scalar2=None, op0=ALU.mult)
+
+        sc0 = const.tile([P, 8, 512], F32, name="sc0")
+        pw = const.tile([P, 3, 8], F32, name="pw")
+        for i in range(8):
+            nc.scalar.activation(out=sc0[:, i, 0:64], in_=niota[:, 0:64], func=ACT.Exp, scale=lsc[:, i : i + 1])
+        for l in range(3):
+            nc.scalar.activation(out=pw[:, l, :], in_=lsc[:], func=ACT.Exp, scale=64.0 * 2**l)
+
+        def scdbl(i):
+            for l in range(3):
+                w = 64 * 2**l
+                nc.scalar.activation(
+                    out=sc0[:, i, w : 2 * w], in_=sc0[:, i, 0:w], func=ACT.Copy, scale=pw[:, l, i : i + 1]
+                )
+
+        trig = const.tile([P, 2, 4, TOK], F32, name="trig")
+        ang3 = const.tile([P, 2], F32, name="ang3")
+
+        def rr(jb):
+            if jb > 0:
+                nc.vector.tensor_scalar(
+                    out=fcol[:, jb : jb + 1], in0=fcol[:, 0:1], scalar1=10000.0 ** (-128.0 * jb / 512.0), scalar2=None, op0=ALU.mult
+                )
+            if jb == 3:
+                nc.vector.tensor_scalar(out=ang3[:, 0:1], in0=fcol[:, 3:4], scalar1=TWO_PI, scalar2=None, op0=ALU.mult)
+                nc.vector.tensor_scalar(out=ang3[:, 1:2], in0=fcol[:, 3:4], scalar1=-TWO_PI, scalar2=None, op0=ALU.mult)
+                return None
+            kk = work.tile([P, TOK], I32, name="kk", tag="kk", bufs=1)
+            nc.vector.tensor_scalar(out=kk[:], in0=niota[:], scalar1=fcol[:, jb : jb + 1], scalar2=None, op0=ALU.mult)
+            nph = work.tile([P, TOK], F32, name="nph", tag="nph", bufs=3)
+            nc.vector.scalar_tensor_tensor(
+                out=nph[:], in0=niota[:], scalar=fcol[:, jb : jb + 1], in1=kk[:], op0=ALU.mult, op1=ALU.subtract
+            )
+            return nph
+
+        def trig_s(jb, nph):
+            cos_t = trig[:, 0, jb, :]
+            sin_t = trig[:, 1, jb, :]
+            if jb == 3:
+                nc.scalar.activation(out=sin_t, in_=niota[:], func=ACT.Sin, scale=ang3[:, 0:1])
+                nc.scalar.activation(out=cos_t, in_=niota[:], func=ACT.Sin, scale=ang3[:, 1:2], bias=halfpi[:])
+                return
+            nc.scalar.activation(out=sin_t, in_=nph[:], func=ACT.Sin, scale=TWO_PI)
+            ab = work.tile([P, TOK], F32, name="ab", tag="ab")
+            nc.scalar.activation(out=ab[:], in_=nph[:], func=ACT.Abs)
+            nc.scalar.activation(out=cos_t, in_=ab[:], func=ACT.Sin, scale=-TWO_PI, bias=halfpi[:])
+
+        xcodes = const.tile([P, 2, TOK], U32, name="xcodes", align_bytes=64)
+        xscl = const.tile([P, 2, TOK], U8, name="xscl", align_bytes=64)
+        xg = {}
+
+        def xprep(h, i):
+            if i == 0:
+                for g in range(2):
+                    xg[(h, g)] = work.tile([P, 512, 4], BF16, name="xg%d" % g, tag="xg%d" % g, align_bytes=64)
+            xt = [ps_o.tile([P, 2, 256], F32, name="xt%d" % g, tag="ot") for g in range(2)]
+            for aa in range(2):
+                a = 2 * i + aa
+                xw = work.tile([P, KDIM], BF16, name="xw", tag="xw", bufs=3)
+                nc.vector.tensor_tensor(out=xw[:], in0=xbytes[h][:, a, :].bitcast(FP8), in1=xs[:], op=ALU.mult)
+                words = xw[:].bitcast(F32)
+                for g in range(2):
+                    for u in range(2):
+                        nc.tensor.transpose(
+                            xt[g][:, u, P * aa : P * aa + P], words[:, 256 * g + u : 256 * (g + 1) : 2], ident[:]
+                        )
+            for g in range(2):
+                gw = xg[(h, g)][:].rearrange("p r t -> p (r t)").bitcast(F32).rearrange("p (r u) -> p r u", u=2)
+                nc.scalar.copy(out=gw[:, 256 * i : 256 * i + 256, :], in_=xt[g][:].rearrange("p u r -> p r u"))
+
+        def xquant(h):
+            for g in range(2):
+                cols = slice(512 * h, 512 * h + 512)
+                nc.vector.quantize_mx(
+                    out=xcodes[:, g, cols].bitcast(FP8X4),
+                    scales=xscl[:, g, cols],
+                    in_=xg[(h, g)][:].rearrange("p r t -> p (r t)"),
+                )
+
+        wcodes = const.tile([P, 2, 4, 512], U32, name="wcodes", align_bytes=64)
+        wscl = const.tile([P, 2, 4, 512], U8, name="wscl", align_bytes=64)
+
+        def wprep(o, jb):
+            wg = work.tile([P, 2, 2, P, 4], BF16, name="wg", tag="wg", align_bytes=64)
+            for g in range(2):
+                src = wraw[(o, jb // 2, g)][:, :, 256 * (jb % 2) : 256 * (jb % 2) + 256].rearrange(
+                    "p t (j e) -> p e j t", e=2
+                )
+                if (o, jb, g) in WIL_ON_V:
+                    nc.vector.tensor_copy(out=wg[:, g, :, :, :], in_=src)
+                else:
+                    nc.scalar.copy(out=wg[:, g, :, :, :], in_=src)
+            nc.vector.quantize_mx(
+                out=wcodes[:, o, jb, :].bitcast(FP8X4),
+                scales=wscl[:, o, jb, :],
+                in_=wg[:].rearrange("p g e j t -> p (g e j t)"),
+            )
+
+        tabs = {}
+        banks = {}
+        gfac = const.tile([P, 4, 4], F32, name="gfac")
+
+        def make_gfac():
+            nc.vector.tensor_copy(out=gfac[:, 0, :], in_=zcol[:])
+            nc.vector.tensor_scalar(out=gfac[:, 1, :], in0=zcol[:], scalar1=-1.0, scalar2=None, op0=ALU.mult)
+            nc.vector.reciprocal(out=gfac[:, 2, :], in_=zcol[:])
+            nc.vector.tensor_scalar(out=gfac[:, 3, :], in0=gfac[:, 2, :], scalar1=-1.0, scalar2=None, op0=ALU.mult)
+
+        def prod(u):
+            o, jb, h = u
+            ct = work.tile([P, 512], F32, name="ct", tag="ct", bufs=3)
+            st = work.tile([P, 512], F32, name="st", tag="st", bufs=3)
+            hs = slice(512 * h, 512 * h + 512)
+            nc.gpsimd.tensor_tensor(out=ct[:], in0=trig[:, 0, jb, hs], in1=sc0[:, 4 * o + jb, :], op=ALU.mult)
+            nc.gpsimd.tensor_tensor(out=st[:], in0=trig[:, 1, jb, hs], in1=sc0[:, 4 * o + jb, :], op=ALU.mult)
+            tabs[u] = (ct, st)
+
+        def mx_passes(u):
+            o, jb, h = u
+            pp = []
+            calls = []
+            for e in range(2):
+                acc = ps_p.tile([P, 512], F32, name="acc%d" % e, tag="acc%d" % e)
+                pp.append(acc)
+                for g in range(2):
+                    calls.append((acc, e, g))
+            banks[u] = pp
+
+            def one(c):
+                acc, e, g = c
+                wc = slice(256 * g + P * e, 256 * g + P * e + P)
+                xc = slice(512 * h, 512 * h + 512)
+                nc.tensor.matmul_mx(
+                    out=acc[:],
+                    lhsT=wcodes[:, o, jb, wc].bitcast(FP8X4),
+                    lhsT_scale=wscl[:, o, jb, wc],
+                    rhs=xcodes[:, g, xc].bitcast(FP8X4),
+                    rhs_scale=xscl[:, g, xc],
+                    start=(g == 0),
+                    stop=(g == 1),
+                )
+
+            return [(one, c) for c in calls]
+
+        prods = {}
+
+        def epi_v(u, pieces):
+            o, jb, h = u
+            pe, po = banks[u]
+            ct, st = tabs[u]
+            if h == 0:
+                gp, gn = 1.0, -1.0
+            else:
+                gp = gfac[:, 2 * o, jb : jb + 1]
+                gn = gfac[:, 2 * o + 1, jb : jb + 1]
+            ms = {}
+            for idx in range(4):
+                ms[idx] = work.tile([P, 512], F32, name="m%d" % idx, tag="m%d" % idx, bufs=3)
+            w = 512 // pieces
+            for piece in range(pieces):
+                cs = slice(w * piece, w * piece + w)
+                for idx, src, g, tab in ((0, pe, gp, ct), (3, pe, gp, st), (2, po, gp, ct), (1, po, gn, st)):
+                    nc.vector.scalar_tensor_tensor(
+                        out=ms[idx][:, cs], in0=tab[:, cs], scalar=g, in1=src[:, cs], op0=ALU.mult, op1=ALU.mult
+                    )
+            prods[u] = ms
+
+        def pe_block(u_t, u_mx):
+            passes = mx_passes(u_mx) if u_mx is not None else []
+            last = u_t is not None and u_mx is None
+            ots = []
+            if u_t is not None:
+                ms = prods[u_t]
+                for b in range(2):
+                    ot = ps_o.tile([P, 2, 2, P], F32, name="ot", tag="ot")
+                    ots.append(ot)
+            for r in range(2):
+                for fn, c in passes[2 * r : 2 * r + 2]:
+                    fn(c)
+                if u_t is not None:
+                    if last:
+                        todo = [(r, s, e, z) for e in range(2) for s in range(2) for z in range(2)]
+                    else:
+                        todo = [(s, r, e, z) for e in range(2) for z in range(2) for s in range(2)]
+                    for b, qq, e, z in todo:
+                        q = 2 * b + qq
+                        nc.tensor.matmul(
+                            out=ots[b][:, qq, e, :], lhsT=ms[2 * e + z][:, P * q : P * q + P], rhs=ident[:],
+                            is_transpose=True, start=(z == 0), stop=(z == 1),
+                        )
+            return ots
+
+        def evac(u, ots):
+            o, jb, h = u
+            for b in range(2):
+                sg = work.tile([P, 2, 256], F32, name="stg%d" % b, tag="stg%d" % b, bufs=3)
+                nc.scalar.copy(
+                    out=sg[:].rearrange("p q (j e) -> p q j e", e=2),
+                    in_=ots[b][:].rearrange("p q e j -> p q j e"),
+                )
+                t0 = 4 * h + 2 * b
+                nc.sync.dma_start(out=outs[o][:, t0 : t0 + 2, 256 * jb : 256 * jb + 256], in_=sg[:])
+
+        pairs = [(o, jb) for o in range(2) for jb in range(4)]
+        units = [(o, jb, h) for (o, jb) in pairs for h in range(2)]
+        n_units = len(units)
+
+        def pair_prep(k):
+            o, jb = pairs[k]
+            if o == 0:
+                trig_s(jb, nphs[jb])
+            scdbl(4 * o + jb)
+            wprep(o, jb)
+
+        nphs = [rr(jb) for jb in range(4)]
+        trig_s(0, nphs[0])
+        scdbl(0)
+        xprep(0, 0)
+        xprep(0, 1)
+        xquant(0)
+        wprep(0, 0)
+        prod(units[0])
+        pe_block(None, units[0])
+        xprep(1, 0)
+        xprep(1, 1)
+        xquant(1)
+        prod(units[1])
+        make_gfac()
+        for n in range(n_units + 1):
+            if n % 2 == 0 and n // 2 + 1 < len(pairs):
+                pair_prep(n // 2 + 1)
+            if n == 0:
+                load_w(1, 1)
+            if n + 2 < n_units:
+                prod(units[n + 2])
+            ots = pe_block(units[n - 1] if n >= 1 else None, units[n + 1] if n + 1 < n_units else None)
+            if n < n_units:
+                epi_v(units[n], 2 if n == n_units - 1 else 1)
+            if n >= 1:
+                evac(units[n - 1], ots)

@@ -50,7 +50,7 @@ def tile_simpleretention_pa_kernel(tc, X_bytes, X_scale, W_Q, W_K, out_0, out_1)
 
         def load_w(o, c):
             for g in range(2):
-                t = work.tile([P, 4, 512], BF16, name="wraw", tag="wraw", bufs=6)
+                t = work.tile([P, 4, 512], BF16, name="wraw", tag="wraw", bufs=8)
                 wraw[(o, c, g)] = t
                 nc.sync.dma_start(
                     out=t[:],
@@ -62,8 +62,9 @@ def tile_simpleretention_pa_kernel(tc, X_bytes, X_scale, W_Q, W_K, out_0, out_1)
         load_x(0)
         load_w(0, 0)
         load_x(1)
-        load_w(0, 1)
         load_w(1, 0)
+        load_w(0, 1)
+        load_w(1, 1)
 
         ones = const.tile([P, 16], F32, name="ones")
         nc.vector.memset(ones[:], 1.0)
@@ -307,16 +308,9 @@ def tile_simpleretention_pa_kernel(tc, X_bytes, X_scale, W_Q, W_K, out_0, out_1)
                 t0 = 4 * h + 2 * b
                 nc.sync.dma_start(out=outs[o][:, t0 : t0 + 2, 256 * jb : 256 * jb + 256], in_=sg[:])
 
-        pairs = [(o, jb) for o in range(2) for jb in range(4)]
+        pairs = [(o, jb) for jb in range(4) for o in range(2)]
         units = [(o, jb, h) for (o, jb) in pairs for h in range(2)]
         n_units = len(units)
-
-        def pair_prep(k):
-            o, jb = pairs[k]
-            if o == 0:
-                trig_s(jb, nphs[jb])
-            scdbl(4 * o + jb)
-            wprep(o, jb)
 
         nphs = [rr(jb) for jb in range(4)]
         trig_s(0, nphs[0])
@@ -333,10 +327,15 @@ def tile_simpleretention_pa_kernel(tc, X_bytes, X_scale, W_Q, W_K, out_0, out_1)
         prod(units[1])
         make_gfac()
         for n in range(n_units + 1):
-            if n % 2 == 0 and n // 2 + 1 < len(pairs):
-                pair_prep(n // 2 + 1)
-            if n == 0:
-                load_w(1, 1)
+            jb_now = n // 4
+            if n % 4 == 0 and jb_now < 4:
+                scdbl(4 + jb_now)
+                wprep(1, jb_now)
+            if n % 4 == 1 and jb_now + 1 < 4:
+                trig_s(jb_now + 1, nphs[jb_now + 1])
+            if n % 4 == 2 and jb_now + 1 < 4:
+                scdbl(jb_now + 1)
+                wprep(0, jb_now + 1)
             if n + 2 < n_units:
                 prod(units[n + 2])
             ots = pe_block(units[n - 1] if n >= 1 else None, units[n + 1] if n + 1 < n_units else None)

@@ -21,7 +21,7 @@ CH = 1024
 FLOPS = 2 * TOK * KDIM * 2 * CH
 
 TWO_PI = 2.0 * math.pi
-WIL_ON_V = ((0, 0, 0), (0, 0, 1))
+JB = (3, 0, 1, 2)
 
 
 def tile_simpleretention_pa_kernel(tc, X_bytes, X_scale, W_Q, W_K, out_0, out_1):
@@ -38,7 +38,7 @@ def tile_simpleretention_pa_kernel(tc, X_bytes, X_scale, W_Q, W_K, out_0, out_1)
         work = ctx.enter_context(tc.tile_pool(name="work", bufs=2))
         ps_p = ctx.enter_context(tc.psum_pool(name="psp", bufs=2))
         ps_o = ctx.enter_context(tc.psum_pool(name="pso", bufs=4))
-        ctx.enter_context(tc.manual_schedule(engines={mybir.EngineType.PE}))
+        ctx.enter_context(tc.manual_schedule())
 
         xs = const.tile([P, KDIM], F32, name="xs")
         nc.scalar.dma_start(out=xs[:], in_=X_scale.rearrange("a b k -> (a b k)").partition_broadcast(P))
@@ -60,30 +60,20 @@ def tile_simpleretention_pa_kernel(tc, X_bytes, X_scale, W_Q, W_K, out_0, out_1)
                 )
 
         load_x(0)
-        load_w(0, 0)
-        load_x(1)
-        load_w(1, 0)
         load_w(0, 1)
         load_w(1, 1)
+        load_x(1)
+        load_w(0, 0)
+        load_w(1, 0)
 
         ones = const.tile([P, 16], F32, name="ones")
         nc.vector.memset(ones[:], 1.0)
-        ident = const.tile([P, P], F32, name="ident")
-        make_identity(nc, ident[:])
         jcol = const.tile([P, 4], F32, name="jcol")
         nc.gpsimd.iota(jcol[:], pattern=[[P, 4]], base=0, channel_multiplier=1, allow_small_or_imprecise_dtypes=True)
+        ident = const.tile([P, P], F32, name="ident")
+        make_identity(nc, ident[:])
         niota = const.tile([P, TOK], F32, name="niota")
         nc.gpsimd.iota(niota[:], pattern=[[1, TOK]], base=0, channel_multiplier=0, allow_small_or_imprecise_dtypes=True)
-
-        zcol = const.tile([P, 4], F32, name="zcol")
-        nc.vector.tensor_scalar(
-            out=zcol[:], in0=jcol[:], scalar1=2.0 / (1.4 * 1024), scalar2=(0.4 * 1024) / (1.4 * 1024), op0=ALU.mult, op1=ALU.add
-        )
-        lnz = const.tile([P, 4], F32, name="lnz")
-        nc.scalar.activation(out=lnz[:], in_=zcol[:], func=ACT.Ln)
-        lsc = const.tile([P, 8], F32, name="lsc")
-        nc.vector.tensor_scalar(out=lsc[:, 0:4], in0=lnz[:], scalar1=1.0 / 512.0, scalar2=None, op0=ALU.mult)
-        nc.vector.tensor_scalar(out=lsc[:, 4:8], in0=lnz[:], scalar1=-1.0 / 512.0, scalar2=None, op0=ALU.mult)
 
         vv = const.tile([P, 16], F32, name="vv")
         for b in range(16):
@@ -101,10 +91,20 @@ def tile_simpleretention_pa_kernel(tc, X_bytes, X_scale, W_Q, W_K, out_0, out_1)
             )
         rt = ps_o.tile([P, 512], F32, name="rt", tag="ot")
         nc.tensor.transpose(rt[:, 0:P], rrow[:], ident[:])
-        fcol = const.tile([P, 4], F32, name="fcol")
-        nc.vector.tensor_copy(out=fcol[:, 0:1], in_=rt[:, 0:1])
+
+        zcol = const.tile([P, 4], F32, name="zcol")
+        nc.vector.tensor_scalar(
+            out=zcol[:], in0=jcol[:], scalar1=2.0 / (1.4 * 1024), scalar2=(0.4 * 1024) / (1.4 * 1024), op0=ALU.mult, op1=ALU.add
+        )
+        lnz = const.tile([P, 4], F32, name="lnz")
+        nc.scalar.activation(out=lnz[:], in_=zcol[:], func=ACT.Ln)
         halfpi = const.tile([P, 1], F32, name="halfpi")
         nc.vector.tensor_scalar(out=halfpi[:], in0=ones[:, 0:1], scalar1=0.5 * math.pi, scalar2=None, op0=ALU.mult)
+        fcol = const.tile([P, 4], F32, name="fcol")
+        nc.vector.tensor_copy(out=fcol[:, 0:1], in_=rt[:, 0:1])
+        lsc = const.tile([P, 8], F32, name="lsc")
+        nc.vector.tensor_scalar(out=lsc[:, 0:4], in0=lnz[:], scalar1=1.0 / 512.0, scalar2=None, op0=ALU.mult)
+        nc.vector.tensor_scalar(out=lsc[:, 4:8], in0=lnz[:], scalar1=-1.0 / 512.0, scalar2=None, op0=ALU.mult)
 
         sc0 = const.tile([P, 8, 512], F32, name="sc0")
         pw = const.tile([P, 3, 8], F32, name="pw")
@@ -122,8 +122,10 @@ def tile_simpleretention_pa_kernel(tc, X_bytes, X_scale, W_Q, W_K, out_0, out_1)
 
         trig = const.tile([P, 2, 4, TOK], F32, name="trig")
         ang3 = const.tile([P, 2], F32, name="ang3")
+        kks = {}
+        nphs = {}
 
-        def rr(jb):
+        def rr_a(jb):
             if jb > 0:
                 nc.vector.tensor_scalar(
                     out=fcol[:, jb : jb + 1], in0=fcol[:, 0:1], scalar1=10000.0 ** (-128.0 * jb / 512.0), scalar2=None, op0=ALU.mult
@@ -131,22 +133,26 @@ def tile_simpleretention_pa_kernel(tc, X_bytes, X_scale, W_Q, W_K, out_0, out_1)
             if jb == 3:
                 nc.vector.tensor_scalar(out=ang3[:, 0:1], in0=fcol[:, 3:4], scalar1=TWO_PI, scalar2=None, op0=ALU.mult)
                 nc.vector.tensor_scalar(out=ang3[:, 1:2], in0=fcol[:, 3:4], scalar1=-TWO_PI, scalar2=None, op0=ALU.mult)
-                return None
+                return
             kk = work.tile([P, TOK], I32, name="kk", tag="kk", bufs=1)
             nc.vector.tensor_scalar(out=kk[:], in0=niota[:], scalar1=fcol[:, jb : jb + 1], scalar2=None, op0=ALU.mult)
-            nph = work.tile([P, TOK], F32, name="nph", tag="nph", bufs=3)
-            nc.vector.scalar_tensor_tensor(
-                out=nph[:], in0=niota[:], scalar=fcol[:, jb : jb + 1], in1=kk[:], op0=ALU.mult, op1=ALU.subtract
-            )
-            return nph
+            kks[jb] = kk
 
-        def trig_s(jb, nph):
+        def rr_b(jb):
+            nph = work.tile([P, TOK], F32, name="nph", tag="nph", bufs=2)
+            nc.vector.scalar_tensor_tensor(
+                out=nph[:], in0=niota[:], scalar=fcol[:, jb : jb + 1], in1=kks[jb][:], op0=ALU.mult, op1=ALU.subtract
+            )
+            nphs[jb] = nph
+
+        def trig_s(jb):
             cos_t = trig[:, 0, jb, :]
             sin_t = trig[:, 1, jb, :]
             if jb == 3:
                 nc.scalar.activation(out=sin_t, in_=niota[:], func=ACT.Sin, scale=ang3[:, 0:1])
                 nc.scalar.activation(out=cos_t, in_=niota[:], func=ACT.Sin, scale=ang3[:, 1:2], bias=halfpi[:])
                 return
+            nph = nphs[jb]
             nc.scalar.activation(out=sin_t, in_=nph[:], func=ACT.Sin, scale=TWO_PI)
             ab = work.tile([P, TOK], F32, name="ab", tag="ab")
             nc.scalar.activation(out=ab[:], in_=nph[:], func=ACT.Abs)
@@ -186,21 +192,23 @@ def tile_simpleretention_pa_kernel(tc, X_bytes, X_scale, W_Q, W_K, out_0, out_1)
 
         wcodes = const.tile([P, 2, 4, 512], U32, name="wcodes", align_bytes=64)
         wscl = const.tile([P, 2, 4, 512], U8, name="wscl", align_bytes=64)
+        wgs = {}
 
-        def wprep(o, jb):
-            wg = work.tile([P, 2, 2, P, 4], BF16, name="wg", tag="wg", align_bytes=64)
-            for g in range(2):
-                src = wraw[(o, jb // 2, g)][:, :, 256 * (jb % 2) : 256 * (jb % 2) + 256].rearrange(
-                    "p t (j e) -> p e j t", e=2
-                )
-                if (o, jb, g) in WIL_ON_V:
-                    nc.vector.tensor_copy(out=wg[:, g, :, :, :], in_=src)
-                else:
-                    nc.scalar.copy(out=wg[:, g, :, :, :], in_=src)
+        def wil(o, jb, g, on_vector=False):
+            if g == 0:
+                wgs[(o, jb)] = work.tile([P, 2, 2, P, 4], BF16, name="wg", tag="wg", align_bytes=64)
+            wg = wgs[(o, jb)]
+            src = wraw[(o, jb // 2, g)][:, :, 256 * (jb % 2) : 256 * (jb % 2) + 256].rearrange("p t (j e) -> p e j t", e=2)
+            if on_vector:
+                nc.vector.tensor_copy(out=wg[:, g, :, :, :], in_=src)
+            else:
+                nc.scalar.copy(out=wg[:, g, :, :, :], in_=src)
+
+        def wquant(o, jb):
             nc.vector.quantize_mx(
                 out=wcodes[:, o, jb, :].bitcast(FP8X4),
                 scales=wscl[:, o, jb, :],
-                in_=wg[:].rearrange("p g e j t -> p (g e j t)"),
+                in_=wgs[(o, jb)][:].rearrange("p g e j t -> p (g e j t)"),
             )
 
         tabs = {}
@@ -272,7 +280,7 @@ def tile_simpleretention_pa_kernel(tc, X_bytes, X_scale, W_Q, W_K, out_0, out_1)
                     )
             prods[u] = ms
 
-        def pe_block(u_t, u_mx):
+        def pe_block(u_t, u_mx, t_first=False):
             passes = mx_passes(u_mx) if u_mx is not None else []
             last = u_t is not None and u_mx is None
             ots = []
@@ -282,8 +290,9 @@ def tile_simpleretention_pa_kernel(tc, X_bytes, X_scale, W_Q, W_K, out_0, out_1)
                     ot = ps_o.tile([P, 2, 2, P], F32, name="ot", tag="ot")
                     ots.append(ot)
             for r in range(2):
-                for fn, c in passes[2 * r : 2 * r + 2]:
-                    fn(c)
+                if not t_first:
+                    for fn, c in passes[2 * r : 2 * r + 2]:
+                        fn(c)
                 if u_t is not None:
                     if last:
                         todo = [(r, s, e, z) for e in range(2) for s in range(2) for z in range(2)]
@@ -295,6 +304,9 @@ def tile_simpleretention_pa_kernel(tc, X_bytes, X_scale, W_Q, W_K, out_0, out_1)
                             out=ots[b][:, qq, e, :], lhsT=ms[2 * e + z][:, P * q : P * q + P], rhs=ident[:],
                             is_transpose=True, start=(z == 0), stop=(z == 1),
                         )
+                if t_first:
+                    for fn, c in passes[2 * r : 2 * r + 2]:
+                        fn(c)
             return ots
 
         def evac(u, ots):
@@ -308,38 +320,83 @@ def tile_simpleretention_pa_kernel(tc, X_bytes, X_scale, W_Q, W_K, out_0, out_1)
                 t0 = 4 * h + 2 * b
                 nc.sync.dma_start(out=outs[o][:, t0 : t0 + 2, 256 * jb : 256 * jb + 256], in_=sg[:])
 
-        pairs = [(o, jb) for jb in range(4) for o in range(2)]
-        units = [(o, jb, h) for (o, jb) in pairs for h in range(2)]
+        units = [(0, JB[0], 0), (1, JB[0], 0), (0, JB[0], 1), (1, JB[0], 1)]
+        units += [(o, jb, h) for jb in JB[1:] for o in range(2) for h in range(2)]
         n_units = len(units)
 
-        nphs = [rr(jb) for jb in range(4)]
-        trig_s(0, nphs[0])
-        scdbl(0)
+        def preps_s(n):
+            c, r = n // 4, n % 4
+            if c + 1 >= 4:
+                return
+            nxt = JB[c + 1]
+            if r == 0:
+                trig_s(nxt)
+            if r == 1:
+                scdbl(nxt)
+                wil(0, nxt, 0)
+                wil(0, nxt, 1)
+            if r == 2:
+                scdbl(4 + nxt)
+                wil(1, nxt, 0)
+            if r == 3:
+                wil(1, nxt, 1)
+
+        def preps_v(n):
+            c, r = n // 4, n % 4
+            if r == 0 and 1 <= c < 4:
+                wquant(1, JB[c])
+            if r == 1 and c + 2 < 4:
+                rr_a(JB[c + 2])
+            if r == 2 and c + 1 < 4:
+                wquant(0, JB[c + 1])
+            if r == 3 and c + 2 < 4:
+                rr_b(JB[c + 2])
+
+        rr_a(JB[0])
+        trig_s(JB[0])
+        scdbl(JB[0])
+        scdbl(4 + JB[0])
+        make_gfac()
+        rr_a(JB[1])
+        rr_b(JB[1])
+        wil(0, JB[0], 0, on_vector=True)
+        wil(0, JB[0], 1, on_vector=True)
+        wquant(0, JB[0])
         xprep(0, 0)
         xprep(0, 1)
         xquant(0)
-        wprep(0, 0)
         prod(units[0])
-        pe_block(None, units[0])
-        xprep(1, 0)
-        xprep(1, 1)
-        xquant(1)
         prod(units[1])
-        make_gfac()
-        for n in range(n_units + 1):
-            jb_now = n // 4
-            if n % 4 == 0 and jb_now < 4:
-                scdbl(4 + jb_now)
-                wprep(1, jb_now)
-            if n % 4 == 1 and jb_now + 1 < 4:
-                trig_s(jb_now + 1, nphs[jb_now + 1])
-            if n % 4 == 2 and jb_now + 1 < 4:
-                scdbl(jb_now + 1)
-                wprep(0, jb_now + 1)
+        pe_block(None, units[0])
+        wil(1, JB[0], 0)
+        wil(1, JB[0], 1)
+        xprep(1, 0)
+        wquant(1, JB[0])
+        pe_block(None, units[1])
+        preps_s(0)
+        prod(units[2])
+        epi_v(units[0], 1)
+        ots = pe_block(units[0], None, t_first=True)
+        xprep(1, 1)
+        evac(units[0], ots)
+        preps_s(1)
+        prod(units[3])
+        epi_v(units[1], 1)
+        xquant(1)
+        ots = pe_block(units[1], units[2], t_first=True)
+        pe_block(None, units[3])
+        evac(units[1], ots)
+        preps_s(2)
+        prod(units[4])
+        epi_v(units[2], 1)
+        preps_v(2)
+        preps_v(1)
+        for n in range(3, n_units + 1):
+            preps_s(n)
             if n + 2 < n_units:
                 prod(units[n + 2])
-            ots = pe_block(units[n - 1] if n >= 1 else None, units[n + 1] if n + 1 < n_units else None)
+            ots = pe_block(units[n - 1], units[n + 1] if n + 1 < n_units else None)
             if n < n_units:
                 epi_v(units[n], 2 if n == n_units - 1 else 1)
-            if n >= 1:
-                evac(units[n - 1], ots)
+                preps_v(n)
+            evac(units[n - 1], ots)

@@ -120,7 +120,7 @@ def tile_simpleretention_pa_kernel(tc, X_bytes, X_scale, W_Q, W_K, out_0, out_1)
                     out=sc0[:, i, w : 2 * w], in_=sc0[:, i, 0:w], func=ACT.Copy, scale=pw[:, l, i : i + 1]
                 )
 
-        trig = const.tile([P, 2, 4, TOK], F32, name="trig")
+        trig = const.tile([P, 4, 2, TOK], F32, name="trig")
         ang3 = const.tile([P, 2], F32, name="ang3")
         kks = {}
         nphs = {}
@@ -146,8 +146,8 @@ def tile_simpleretention_pa_kernel(tc, X_bytes, X_scale, W_Q, W_K, out_0, out_1)
             nphs[jb] = nph
 
         def trig_s(jb):
-            cos_t = trig[:, 0, jb, :]
-            sin_t = trig[:, 1, jb, :]
+            cos_t = trig[:, jb, 0, :]
+            sin_t = trig[:, jb, 1, :]
             if jb == 3:
                 nc.scalar.activation(out=sin_t, in_=niota[:], func=ACT.Sin, scale=ang3[:, 0:1])
                 nc.scalar.activation(out=cos_t, in_=niota[:], func=ACT.Sin, scale=ang3[:, 1:2], bias=halfpi[:])
@@ -221,14 +221,16 @@ def tile_simpleretention_pa_kernel(tc, X_bytes, X_scale, W_Q, W_K, out_0, out_1)
             nc.vector.reciprocal(out=gfac[:, 2, :], in_=zcol[:])
             nc.vector.tensor_scalar(out=gfac[:, 3, :], in0=gfac[:, 2, :], scalar1=-1.0, scalar2=None, op0=ALU.mult)
 
-        def prod(u):
+        def prod(u, eng):
             o, jb, h = u
-            ct = work.tile([P, 512], F32, name="ct", tag="ct", bufs=3)
-            st = work.tile([P, 512], F32, name="st", tag="st", bufs=3)
-            hs = slice(512 * h, 512 * h + 512)
-            nc.gpsimd.tensor_tensor(out=ct[:], in0=trig[:, 0, jb, hs], in1=sc0[:, 4 * o + jb, :], op=ALU.mult)
-            nc.gpsimd.tensor_tensor(out=st[:], in0=trig[:, 1, jb, hs], in1=sc0[:, 4 * o + jb, :], op=ALU.mult)
-            tabs[u] = (ct, st)
+            tb = work.tile([P, 2, 512], F32, name="tb", tag="tb", bufs=2)
+            eng.tensor_tensor(
+                out=tb[:],
+                in0=trig[:, jb, :, 512 * h : 512 * h + 512],
+                in1=sc0[:, 4 * o + jb, :].unsqueeze(1).to_broadcast([P, 2, 512]),
+                op=ALU.mult,
+            )
+            tabs[u] = (tb[:, 0, :], tb[:, 1, :])
 
         def mx_passes(u):
             o, jb, h = u
@@ -259,7 +261,7 @@ def tile_simpleretention_pa_kernel(tc, X_bytes, X_scale, W_Q, W_K, out_0, out_1)
 
         prods = {}
 
-        def epi_v(u, pieces):
+        def epi_v(u, pieces, ports=None):
             o, jb, h = u
             pe, po = banks[u]
             ct, st = tabs[u]
@@ -275,6 +277,8 @@ def tile_simpleretention_pa_kernel(tc, X_bytes, X_scale, W_Q, W_K, out_0, out_1)
             for piece in range(pieces):
                 cs = slice(w * piece, w * piece + w)
                 for idx, src, g, tab in ((0, pe, gp, ct), (3, pe, gp, st), (2, po, gp, ct), (1, po, gn, st)):
+                    if idx == 1 and ports is not None:
+                        ports()
                     nc.vector.scalar_tensor_tensor(
                         out=ms[idx][:, cs], in0=tab[:, cs], scalar=g, in1=src[:, cs], op0=ALU.mult, op1=ALU.mult
                     )
@@ -364,9 +368,9 @@ def tile_simpleretention_pa_kernel(tc, X_bytes, X_scale, W_Q, W_K, out_0, out_1)
         wquant(0, JB[0])
         xprep(0, 0)
         xprep(0, 1)
+        prod(units[0], nc.vector)
+        prod(units[1], nc.vector)
         xquant(0)
-        prod(units[0])
-        prod(units[1])
         pe_block(None, units[0])
         wil(1, JB[0], 0)
         wil(1, JB[0], 1)
@@ -374,29 +378,31 @@ def tile_simpleretention_pa_kernel(tc, X_bytes, X_scale, W_Q, W_K, out_0, out_1)
         wquant(1, JB[0])
         pe_block(None, units[1])
         preps_s(0)
-        prod(units[2])
-        epi_v(units[0], 1)
+        epi_v(units[0], 1, lambda: xprep(1, 1))
+        prod(units[2], nc.gpsimd)
         ots = pe_block(units[0], None, t_first=True)
-        xprep(1, 1)
         evac(units[0], ots)
         preps_s(1)
-        prod(units[3])
-        epi_v(units[1], 1)
-        xquant(1)
+        epi_v(units[1], 1, lambda: xquant(1))
+        prod(units[3], nc.gpsimd)
         ots = pe_block(units[1], units[2], t_first=True)
         pe_block(None, units[3])
         evac(units[1], ots)
         preps_s(2)
-        prod(units[4])
-        epi_v(units[2], 1)
-        preps_v(2)
-        preps_v(1)
+
+        def ports2():
+            preps_v(2)
+            preps_v(1)
+
+        epi_v(units[2], 1, ports2)
+        prod(units[4], nc.gpsimd)
         for n in range(3, n_units + 1):
             preps_s(n)
-            if n + 2 < n_units:
-                prod(units[n + 2])
             ots = pe_block(units[n - 1], units[n + 1] if n + 1 < n_units else None)
-            if n < n_units:
-                epi_v(units[n], 2 if n == n_units - 1 else 1)
-                preps_v(n)
+            if n == n_units - 1:
+                epi_v(units[n], 2)
+            elif n < n_units:
+                epi_v(units[n], 1, lambda: preps_v(n))
+            if n + 2 < n_units:
+                prod(units[n + 2], nc.gpsimd)
             evac(units[n - 1], ots)

@@ -48,23 +48,24 @@ def tile_simpleretention_pa_kernel(tc, X_bytes, X_scale, W_Q, W_K, out_0, out_1)
         def load_x(h):
             nc.sync.dma_start(out=xbytes[h][:], in_=xb_view[:, 4 * h : 4 * h + 4, :])
 
-        def load_w(o, c):
+        def load_w(o, jb):
             for g in range(2):
-                t = work.tile([P, 4, 512], BF16, name="wraw", tag="wraw", bufs=8)
-                wraw[(o, c, g)] = t
+                t = work.tile([P, 4, 256], BF16, name="wraw", tag="wraw", bufs=16)
+                wraw[(o, jb, g)] = t
                 nc.sync.dma_start(
                     out=t[:],
-                    in_=weights[o][512 * g : 512 * (g + 1), 512 * c : 512 * (c + 1)].rearrange(
+                    in_=weights[o][512 * g : 512 * (g + 1), 256 * jb : 256 * (jb + 1)].rearrange(
                         "(p t) n -> p t n", t=4
                     ),
                 )
 
+        load_w(0, JB[0])
         load_x(0)
-        load_w(0, 1)
-        load_w(1, 1)
+        load_w(1, JB[0])
         load_x(1)
-        load_w(0, 0)
-        load_w(1, 0)
+        for jb in JB[1:]:
+            load_w(0, jb)
+            load_w(1, jb)
 
         ones = const.tile([P, 16], F32, name="ones")
         nc.vector.memset(ones[:], 1.0)
@@ -198,7 +199,7 @@ def tile_simpleretention_pa_kernel(tc, X_bytes, X_scale, W_Q, W_K, out_0, out_1)
             if g == 0:
                 wgs[(o, jb)] = work.tile([P, 2, 2, P, 4], BF16, name="wg", tag="wg", align_bytes=64)
             wg = wgs[(o, jb)]
-            src = wraw[(o, jb // 2, g)][:, :, 256 * (jb % 2) : 256 * (jb % 2) + 256].rearrange("p t (j e) -> p e j t", e=2)
+            src = wraw[(o, jb, g)][:].rearrange("p t (j e) -> p e j t", e=2)
             if on_vector:
                 nc.vector.tensor_copy(out=wg[:, g, :, :, :], in_=src)
             else:
@@ -334,11 +335,11 @@ def tile_simpleretention_pa_kernel(tc, X_bytes, X_scale, W_Q, W_K, out_0, out_1)
                 return
             nxt = JB[c + 1]
             if r == 0:
-                trig_s(nxt)
-            if r == 1:
                 scdbl(nxt)
                 wil(0, nxt, 0)
                 wil(0, nxt, 1)
+            if r == 1:
+                trig_s(nxt)
             if r == 2:
                 scdbl(4 + nxt)
                 wil(1, nxt, 0)
@@ -385,7 +386,7 @@ def tile_simpleretention_pa_kernel(tc, X_bytes, X_scale, W_Q, W_K, out_0, out_1)
         preps_s(1)
         epi_v(units[1], 1, lambda: xquant(1))
         prod(units[3], nc.gpsimd)
-        ots = pe_block(units[1], units[2], t_first=True)
+        ots = pe_block(units[1], units[2])
         pe_block(None, units[3])
         evac(units[1], ots)
         preps_s(2)

@@ -199,11 +199,13 @@ def tile_simpleretention_pa_kernel(tc, X_bytes, X_scale, W_Q, W_K, out_0, out_1)
             if g == 0:
                 wgs[(o, jb)] = work.tile([P, 2, 2, P, 4], BF16, name="wg", tag="wg", align_bytes=64)
             wg = wgs[(o, jb)]
-            src = wraw[(o, jb, g)][:].rearrange("p t (j e) -> p e j t", e=2)
             if on_vector:
+                src = wraw[(o, jb, g)][:].rearrange("p t (j e) -> p e j t", e=2)
                 nc.vector.tensor_copy(out=wg[:, g, :, :, :], in_=src)
-            else:
-                nc.scalar.copy(out=wg[:, g, :, :, :], in_=src)
+                return
+            src = wraw[(o, jb, g)][:].rearrange("p t (c i e) -> p e c t i", i=4, e=2)
+            for e in range(2):
+                nc.scalar.copy(out=wg[:, g, e, :, :].rearrange("p (c i) t -> p c t i", i=4), in_=src[:, e, :, :, :])
 
         def wquant(o, jb):
             nc.vector.quantize_mx(

@@ -281,7 +281,12 @@ def tile_simpleretention_pa_kernel(tc, X_bytes, X_scale, W_Q, W_K, out_0, out_1)
                 cs = slice(w * piece, w * piece + w)
                 for idx, src, g, tab in ((0, pe, gp, ct), (3, pe, gp, st), (2, po, gp, ct), (1, po, gn, st)):
                     if idx == 1 and ports is not None:
+                        ca = slice(0, 512 - 64)
+                        nc.vector.scalar_tensor_tensor(
+                            out=ms[idx][:, ca], in0=tab[:, ca], scalar=g, in1=src[:, ca], op0=ALU.mult, op1=ALU.mult
+                        )
                         ports()
+                        cs = slice(512 - 64, 512)
                     nc.vector.scalar_tensor_tensor(
                         out=ms[idx][:, cs], in0=tab[:, cs], scalar=g, in1=src[:, cs], op0=ALU.mult, op1=ALU.mult
                     )
@@ -359,6 +364,10 @@ def tile_simpleretention_pa_kernel(tc, X_bytes, X_scale, W_Q, W_K, out_0, out_1)
             if r == 3 and c + 2 < 4:
                 rr_b(JB[c + 2])
 
+        def has_ports(n):
+            c, r = n // 4, n % 4
+            return (r == 0 and 1 <= c) or (r % 2 == 1 and c + 2 < 4) or (r == 2 and c + 1 < 4)
+
         rr_a(JB[0])
         trig_s(JB[0])
         scdbl(JB[0])
@@ -405,7 +414,7 @@ def tile_simpleretention_pa_kernel(tc, X_bytes, X_scale, W_Q, W_K, out_0, out_1)
             if n == n_units - 1:
                 epi_v(units[n], 2)
             elif n < n_units:
-                epi_v(units[n], 1, lambda: preps_v(n))
+                epi_v(units[n], 1, (lambda: preps_v(n)) if has_ports(n) else None)
             if n + 2 < n_units:
                 prod(units[n + 2], nc.gpsimd)
             evac(units[n - 1], ots)

@@ -1,9 +1,7 @@
 from contextlib import ExitStack
 import math
-
 import concourse.mybir as mybir
 from concourse.masks import make_identity
-
 F32 = mybir.dt.float32
 BF16 = mybir.dt.bfloat16
 U8 = mybir.dt.uint8
@@ -13,60 +11,44 @@ FP8 = mybir.dt.float8_e4m3fn
 FP8X4 = mybir.dt.float8_e4m3fn_x4
 ALU = mybir.AluOpType
 ACT = mybir.ActivationFunctionType
-
 P = 128
 TOK = 1024
 KDIM = 1024
+TWO_PI = 2.0 * math.pi
 CH = 1024
 FLOPS = 2 * TOK * KDIM * 2 * CH
-
-TWO_PI = 2.0 * math.pi
 JB = (3, 0, 1, 2)
 
 
 def tile_simpleretention_pa_kernel(tc, X_bytes, X_scale, W_Q, W_K, out_0, out_1):
     nc = tc.nc
     weights = (W_Q, W_K)
-    outs = (
-        out_0.rearrange("b (t p) c -> p (b t) c", p=P),
-        out_1.rearrange("b (t p) c -> p (b t) c", p=P),
-    )
+    outs = (out_0.rearrange("b (t p) c -> p (b t) c", p=P), out_1.rearrange("b (t p) c -> p (b t) c", p=P))
     xb_view = X_bytes.rearrange("b (a p) k -> p (b a) k", p=P)
-
     with ExitStack() as ctx:
         const = ctx.enter_context(tc.tile_pool(name="const", bufs=1))
         work = ctx.enter_context(tc.tile_pool(name="work", bufs=2))
         ps_p = ctx.enter_context(tc.psum_pool(name="psp", bufs=2))
         ps_o = ctx.enter_context(tc.psum_pool(name="pso", bufs=4))
         ctx.enter_context(tc.manual_schedule())
-
-        xs = const.tile([P, KDIM], F32, name="xs")
-        nc.scalar.dma_start(out=xs[:], in_=X_scale.rearrange("a b k -> (a b k)").partition_broadcast(P))
+        xs = const.tile([P, 2, 4], F32, name="xs")
+        nc.scalar.dma_start(out=xs[:], in_=X_scale.rearrange("a b (g p t) -> p (a b g) t", p=P, t=4))
         xbytes = [const.tile([P, 4, KDIM], U8, name="xbytes%d" % h) for h in range(2)]
         wraw = {}
-
         def load_x(h):
             nc.sync.dma_start(out=xbytes[h][:], in_=xb_view[:, 4 * h : 4 * h + 4, :])
-
         def load_w(o, jb):
             for g in range(2):
                 t = work.tile([P, 4, 256], BF16, name="wraw", tag="wraw", bufs=16)
                 wraw[(o, jb, g)] = t
-                nc.sync.dma_start(
-                    out=t[:],
-                    in_=weights[o][512 * g : 512 * (g + 1), 256 * jb : 256 * (jb + 1)].rearrange(
-                        "(p t) n -> p t n", t=4
-                    ),
-                )
-
+                nc.sync.dma_start(out=t[:], in_=weights[o][512 * g : 512 * (g + 1), 256 * jb : 256 * (jb + 1)].rearrange("(p t) n -> p t n", t=4))
         load_w(0, JB[0])
         load_x(0)
-        load_w(1, JB[0])
         load_x(1)
+        load_w(1, JB[0])
         for jb in JB[1:]:
             load_w(0, jb)
             load_w(1, jb)
-
         ones = const.tile([P, 16], F32, name="ones")
         nc.vector.memset(ones[:], 1.0)
         jcol = const.tile([P, 4], F32, name="jcol")
@@ -75,346 +57,227 @@ def tile_simpleretention_pa_kernel(tc, X_bytes, X_scale, W_Q, W_K, out_0, out_1)
         make_identity(nc, ident[:])
         niota = const.tile([P, TOK], F32, name="niota")
         nc.gpsimd.iota(niota[:], pattern=[[1, TOK]], base=0, channel_multiplier=0, allow_small_or_imprecise_dtypes=True)
-
-        vv = const.tile([P, 16], F32, name="vv")
-        for b in range(16):
-            nc.vector.tensor_scalar(
-                out=vv[:, b : b + 1], in0=ones[:, b : b + 1], scalar1=10000.0 ** (-b / 512.0), scalar2=None, op0=ALU.mult
-            )
-        rrow = const.tile([P, P], F32, name="rrow")
-        for a in range(8):
-            nc.vector.tensor_scalar(
-                out=rrow[:, 16 * a : 16 * a + 16],
-                in0=vv[:],
-                scalar1=10000.0 ** (-16.0 * a / 512.0) / TWO_PI,
-                scalar2=None,
-                op0=ALU.mult,
-            )
-        rt = ps_o.tile([P, 512], F32, name="rt", tag="ot")
-        nc.tensor.transpose(rt[:, 0:P], rrow[:], ident[:])
-
         zcol = const.tile([P, 4], F32, name="zcol")
-        nc.vector.tensor_scalar(
-            out=zcol[:], in0=jcol[:], scalar1=2.0 / (1.4 * 1024), scalar2=(0.4 * 1024) / (1.4 * 1024), op0=ALU.mult, op1=ALU.add
-        )
+        nc.vector.tensor_scalar(out=zcol[:], in0=jcol[:], scalar1=2.0 / (1.4 * 1024), scalar2=(0.4 * 1024) / (1.4 * 1024), op0=ALU.mult, op1=ALU.add)
         lnz = const.tile([P, 4], F32, name="lnz")
         nc.scalar.activation(out=lnz[:], in_=zcol[:], func=ACT.Ln)
+        vv = const.tile([P, 16], F32, name="vv")
+        for b in range(16):
+            nc.vector.tensor_scalar(out=vv[:, b : b + 1], in0=ones[:, b : b + 1], scalar1=10000.0 ** (-b / 512.0), scalar2=None, op0=ALU.mult)
+        rrow = const.tile([P, P], F32, name="rrow")
+        for a in range(8):
+            nc.vector.tensor_scalar(out=rrow[:, 16 * a : 16 * a + 16], in0=vv[:], scalar1=10000.0 ** (-16.0 * a / 512.0) / TWO_PI, scalar2=None, op0=ALU.mult)
+        rt = ps_o.tile([P, 512], F32, name="rt", tag="ot")
+        nc.tensor.transpose(rt[:, 0:P], rrow[:], ident[:])
+        lsc = const.tile([P, 8], F32, name="lsc")
+        nc.vector.tensor_scalar(out=lsc[:, 0:4], in0=lnz[:], scalar1=1.0 / 512.0, scalar2=None, op0=ALU.mult)
+        nc.vector.tensor_scalar(out=lsc[:, 4:8], in0=lnz[:], scalar1=-1.0 / 512.0, scalar2=None, op0=ALU.mult)
         halfpi = const.tile([P, 1], F32, name="halfpi")
         nc.vector.tensor_scalar(out=halfpi[:], in0=ones[:, 0:1], scalar1=0.5 * math.pi, scalar2=None, op0=ALU.mult)
         fcol = const.tile([P, 4], F32, name="fcol")
         nc.vector.tensor_copy(out=fcol[:, 0:1], in_=rt[:, 0:1])
-        lsc = const.tile([P, 8], F32, name="lsc")
-        nc.vector.tensor_scalar(out=lsc[:, 0:4], in0=lnz[:], scalar1=1.0 / 512.0, scalar2=None, op0=ALU.mult)
-        nc.vector.tensor_scalar(out=lsc[:, 4:8], in0=lnz[:], scalar1=-1.0 / 512.0, scalar2=None, op0=ALU.mult)
-
+        ang3 = const.tile([P, 2], F32, name="ang3")
+        for jb in range(1, 4):
+            nc.vector.tensor_scalar(out=fcol[:, jb : jb + 1], in0=fcol[:, 0:1], scalar1=10000.0 ** (-128.0 * jb / 512.0), scalar2=None, op0=ALU.mult)
+        nc.vector.tensor_scalar(out=ang3[:, 0:1], in0=fcol[:, 3:4], scalar1=TWO_PI, scalar2=None, op0=ALU.mult)
+        nc.vector.tensor_scalar(out=ang3[:, 1:2], in0=fcol[:, 3:4], scalar1=-TWO_PI, scalar2=None, op0=ALU.mult)
         sc0 = const.tile([P, 8, 512], F32, name="sc0")
         pw = const.tile([P, 3, 8], F32, name="pw")
-        for i in range(8):
-            nc.scalar.activation(out=sc0[:, i, 0:64], in_=niota[:, 0:64], func=ACT.Exp, scale=lsc[:, i : i + 1])
-        for l in range(3):
-            nc.scalar.activation(out=pw[:, l, :], in_=lsc[:], func=ACT.Exp, scale=64.0 * 2**l)
-
-        def scdbl(i):
+        def exps(part):
+            for i in ((3, 7) if part == 0 else (0, 4, 1, 5, 2, 6)):
+                nc.scalar.activation(out=sc0[:, i, 0:64], in_=niota[:, 0:64], func=ACT.Exp, scale=lsc[:, i : i + 1])
+        def pws():
+            for l in range(3):
+                nc.scalar.activation(out=pw[:, l, :], in_=lsc[:], func=ACT.Exp, scale=64.0 * 2**l)
+        def dbl(i):
             for l in range(3):
                 w = 64 * 2**l
-                nc.scalar.activation(
-                    out=sc0[:, i, w : 2 * w], in_=sc0[:, i, 0:w], func=ACT.Copy, scale=pw[:, l, i : i + 1]
-                )
-
+                nc.scalar.activation(out=sc0[:, i, w : 2 * w], in_=sc0[:, i, 0:w], func=ACT.Copy, scale=pw[:, l, i : i + 1])
+        exps(0); exps(1); pws()
         trig = const.tile([P, 4, 2, TOK], F32, name="trig")
-        ang3 = const.tile([P, 2], F32, name="ang3")
-        kks = {}
-        nphs = {}
-
-        def rr_a(jb):
-            if jb > 0:
-                nc.vector.tensor_scalar(
-                    out=fcol[:, jb : jb + 1], in0=fcol[:, 0:1], scalar1=10000.0 ** (-128.0 * jb / 512.0), scalar2=None, op0=ALU.mult
-                )
-            if jb == 3:
-                nc.vector.tensor_scalar(out=ang3[:, 0:1], in0=fcol[:, 3:4], scalar1=TWO_PI, scalar2=None, op0=ALU.mult)
-                nc.vector.tensor_scalar(out=ang3[:, 1:2], in0=fcol[:, 3:4], scalar1=-TWO_PI, scalar2=None, op0=ALU.mult)
-                return
-            kk = work.tile([P, TOK], I32, name="kk", tag="kk", bufs=1)
+        kks = {}; nphs = {}; abss = {}
+        def rra(jb):
+            kk = work.tile([P, TOK], I32, name="kk", tag="kk", bufs=2)
             nc.vector.tensor_scalar(out=kk[:], in0=niota[:], scalar1=fcol[:, jb : jb + 1], scalar2=None, op0=ALU.mult)
             kks[jb] = kk
-
-        def rr_b(jb):
-            nph = work.tile([P, TOK], F32, name="nph", tag="nph", bufs=2)
-            nc.vector.scalar_tensor_tensor(
-                out=nph[:], in0=niota[:], scalar=fcol[:, jb : jb + 1], in1=kks[jb][:], op0=ALU.mult, op1=ALU.subtract
-            )
+        def rrb(jb):
+            nph = work.tile([P, TOK], F32, name="nph", tag="nph", bufs=3)
+            nc.vector.scalar_tensor_tensor(out=nph[:], in0=niota[:], scalar=fcol[:, jb : jb + 1], in1=kks[jb][:], op0=ALU.mult, op1=ALU.subtract)
             nphs[jb] = nph
-
-        def trig_s(jb):
-            cos_t = trig[:, jb, 0, :]
-            sin_t = trig[:, jb, 1, :]
+        def sin(jb):
+            if jb == 3: nc.scalar.activation(out=trig[:, jb, 1, :], in_=niota[:], func=ACT.Sin, scale=ang3[:, 0:1])
+            else: nc.scalar.activation(out=trig[:, jb, 1, :], in_=nphs[jb][:], func=ACT.Sin, scale=TWO_PI)
+        def cos(jb):
             if jb == 3:
-                nc.scalar.activation(out=sin_t, in_=niota[:], func=ACT.Sin, scale=ang3[:, 0:1])
-                nc.scalar.activation(out=cos_t, in_=niota[:], func=ACT.Sin, scale=ang3[:, 1:2], bias=halfpi[:])
+                nc.scalar.activation(out=trig[:, jb, 0, :], in_=niota[:], func=ACT.Sin, scale=ang3[:, 1:2], bias=halfpi[:])
                 return
-            nph = nphs[jb]
-            nc.scalar.activation(out=sin_t, in_=nph[:], func=ACT.Sin, scale=TWO_PI)
             ab = work.tile([P, TOK], F32, name="ab", tag="ab")
-            nc.scalar.activation(out=ab[:], in_=nph[:], func=ACT.Abs)
-            nc.scalar.activation(out=cos_t, in_=ab[:], func=ACT.Sin, scale=-TWO_PI, bias=halfpi[:])
-
-        xcodes = const.tile([P, 2, TOK], U32, name="xcodes", align_bytes=64)
-        xscl = const.tile([P, 2, TOK], U8, name="xscl", align_bytes=64)
-        xg = {}
-
-        def xprep(h, i):
-            if i == 0:
-                for g in range(2):
-                    xg[(h, g)] = work.tile([P, 512, 4], BF16, name="xg%d" % g, tag="xg%d" % g, align_bytes=64)
+            nc.scalar.activation(out=ab[:], in_=nphs[jb][:], func=ACT.Abs)
+            nc.scalar.activation(out=trig[:, jb, 0, :], in_=ab[:], func=ACT.Sin, scale=-TWO_PI, bias=halfpi[:])
+        xcodes = const.tile([P, 2, 2, 512], U32, name="xcodes", align_bytes=64)
+        xscl = const.tile([P, 2, 2, 512], U8, name="xscl", align_bytes=64)
+        xg = {}; xws = {}; xts = {}
+        def cast(h, a):
+            xw = work.tile([P, KDIM], BF16, name="xw", tag="xw", bufs=4)
+            xws[(h, a)] = xw
+            src = xbytes[h][:, a, :].bitcast(FP8)
+            nc.scalar.copy(out=xw[:], in_=src)
+        def xt(h, i):
             xt = [ps_o.tile([P, 2, 256], F32, name="xt%d" % g, tag="ot") for g in range(2)]
+            xts[(h, i)] = xt
             for aa in range(2):
-                a = 2 * i + aa
-                xw = work.tile([P, KDIM], BF16, name="xw", tag="xw", bufs=3)
-                nc.vector.tensor_tensor(out=xw[:], in0=xbytes[h][:, a, :].bitcast(FP8), in1=xs[:], op=ALU.mult)
-                words = xw[:].bitcast(F32)
+                words = xws[(h, 2 * i + aa)][:].bitcast(F32)
                 for g in range(2):
                     for u in range(2):
-                        nc.tensor.transpose(
-                            xt[g][:, u, P * aa : P * aa + P], words[:, 256 * g + u : 256 * (g + 1) : 2], ident[:]
-                        )
-            for g in range(2):
-                gw = xg[(h, g)][:].rearrange("p r t -> p (r t)").bitcast(F32).rearrange("p (r u) -> p r u", u=2)
-                nc.scalar.copy(out=gw[:, 256 * i : 256 * i + 256, :], in_=xt[g][:].rearrange("p u r -> p r u"))
-
-        def xquant(h):
-            for g in range(2):
-                cols = slice(512 * h, 512 * h + 512)
-                nc.vector.quantize_mx(
-                    out=xcodes[:, g, cols].bitcast(FP8X4),
-                    scales=xscl[:, g, cols],
-                    in_=xg[(h, g)][:].rearrange("p r t -> p (r t)"),
-                )
-
+                        nc.tensor.transpose(xt[g][:, u, P * aa : P * aa + P], words[:, 256 * g + u : 256 * (g + 1) : 2], ident[:])
+        def xsc(h, i, g):
+            if h not in xg: xg[h] = work.tile([P, 2, 512, 4], BF16, name="xg", tag="xg", align_bytes=64)
+            nc.vector.tensor_tensor(
+                out=xg[h][:, g, 256 * i : 256 * i + 256, :].rearrange("p r (u e) -> p r u e", e=2),
+                in0=xts[(h, i)][g][:].rearrange("p u r -> p (u r)").bitcast(BF16).rearrange("p (u r e) -> p r u e", u=2, e=2),
+                in1=xs[:, g, :].rearrange("p (u e) -> p u e", e=2).unsqueeze(1).to_broadcast([P, 256, 2, 2]), op=ALU.mult)
+        def xq(h):
+            nc.vector.quantize_mx(out=xcodes[:, h, :, :].rearrange("p g r -> p (g r)").bitcast(FP8X4), scales=xscl[:, h, :, :].rearrange("p g r -> p (g r)"), in_=xg[h][:].rearrange("p g r t -> p (g r t)"))
         wcodes = const.tile([P, 2, 4, 512], U32, name="wcodes", align_bytes=64)
         wscl = const.tile([P, 2, 4, 512], U8, name="wscl", align_bytes=64)
         wgs = {}
-
-        def wil(o, jb, g, on_vector=False):
-            if g == 0:
-                wgs[(o, jb)] = work.tile([P, 2, 2, P, 4], BF16, name="wg", tag="wg", align_bytes=64)
+        def wil(o, jb, g, e="s"):
+            if (o, jb) not in wgs: wgs[(o, jb)] = work.tile([P, 2, 2, P, 4], BF16, name="wg", tag="wg", bufs=3, align_bytes=64)
             wg = wgs[(o, jb)]
-            if on_vector:
-                src = wraw[(o, jb, g)][:].rearrange("p t (j e) -> p e j t", e=2)
-                nc.vector.tensor_copy(out=wg[:, g, :, :, :], in_=src)
-                return
+            src = wraw[(o, jb, g)][:].rearrange("p t (j e) -> p e j t", e=2)
+            if e == "v": nc.vector.tensor_copy(out=wg[:, g, :, :, :], in_=src); return
+            if e == "g": nc.gpsimd.tensor_scalar(out=wg[:, g, :, :, :], in0=src, scalar1=1.0, scalar2=0.0, op0=ALU.mult, op1=ALU.add); return
             src = wraw[(o, jb, g)][:].rearrange("p t (c i e) -> p e c t i", i=4, e=2)
-            for e in range(2):
-                nc.scalar.copy(out=wg[:, g, e, :, :].rearrange("p (c i) t -> p c t i", i=4), in_=src[:, e, :, :, :])
-
-        def wquant(o, jb):
-            nc.vector.quantize_mx(
-                out=wcodes[:, o, jb, :].bitcast(FP8X4),
-                scales=wscl[:, o, jb, :],
-                in_=wgs[(o, jb)][:].rearrange("p g e j t -> p (g e j t)"),
-            )
-
-        tabs = {}
-        banks = {}
+            for ee in range(2):
+                nc.scalar.copy(out=wg[:, g, ee, :, :].rearrange("p (c i) t -> p c t i", i=4), in_=src[:, ee, :, :, :])
+        def wq(o, jb):
+            nc.vector.quantize_mx(out=wcodes[:, o, jb, :].bitcast(FP8X4), scales=wscl[:, o, jb, :], in_=wgs[(o, jb)][:].rearrange("p g e j t -> p (g e j t)"))
+        tabs = {}; banks = {}; prods = {}; otsd = {}
         gfac = const.tile([P, 4, 4], F32, name="gfac")
-
-        def make_gfac():
+        def gf():
             nc.vector.tensor_copy(out=gfac[:, 0, :], in_=zcol[:])
             nc.vector.tensor_scalar(out=gfac[:, 1, :], in0=zcol[:], scalar1=-1.0, scalar2=None, op0=ALU.mult)
             nc.vector.reciprocal(out=gfac[:, 2, :], in_=zcol[:])
             nc.vector.tensor_scalar(out=gfac[:, 3, :], in0=gfac[:, 2, :], scalar1=-1.0, scalar2=None, op0=ALU.mult)
-
-        def prod(u, eng):
-            o, jb, h = u
-            tb = work.tile([P, 2, 512], F32, name="tb", tag="tb", bufs=2)
-            eng.tensor_tensor(
-                out=tb[:],
-                in0=trig[:, jb, :, 512 * h : 512 * h + 512],
-                in1=sc0[:, 4 * o + jb, :].unsqueeze(1).to_broadcast([P, 2, 512]),
-                op=ALU.mult,
-            )
-            tabs[u] = (tb[:, 0, :], tb[:, 1, :])
-
-        def mx_passes(u):
-            o, jb, h = u
-            pp = []
-            calls = []
-            for e in range(2):
-                acc = ps_p.tile([P, 512], F32, name="acc%d" % e, tag="acc%d" % e)
-                pp.append(acc)
-                for g in range(2):
-                    calls.append((acc, e, g))
-            banks[u] = pp
-
-            def one(c):
-                acc, e, g = c
+        def tab(o, jb, h):
+            tb = work.tile([P, 2, 512], F32, name="tb", tag="tb", bufs=3)
+            nc.gpsimd.tensor_tensor(out=tb[:], in0=trig[:, jb, :, 512 * h : 512 * h + 512], in1=sc0[:, 4 * o + jb, :].unsqueeze(1).to_broadcast([P, 2, 512]), op=ALU.mult)
+            tabs[(o, jb, h)] = (tb[:, 0, :], tb[:, 1, :])
+        def mx(o, jb, h, e):
+            u = (o, jb, h)
+            if u not in banks: banks[u] = {}
+            acc = ps_p.tile([P, 512], F32, name="acc%d" % e, tag="acc%d" % e)
+            banks[u][e] = acc
+            for g in range(2):
                 wc = slice(256 * g + P * e, 256 * g + P * e + P)
-                xc = slice(512 * h, 512 * h + 512)
-                nc.tensor.matmul_mx(
-                    out=acc[:],
-                    lhsT=wcodes[:, o, jb, wc].bitcast(FP8X4),
-                    lhsT_scale=wscl[:, o, jb, wc],
-                    rhs=xcodes[:, g, xc].bitcast(FP8X4),
-                    rhs_scale=xscl[:, g, xc],
-                    start=(g == 0),
-                    stop=(g == 1),
-                )
-
-            return [(one, c) for c in calls]
-
-        prods = {}
-
-        def epi_v(u, pieces, ports=None):
-            o, jb, h = u
-            pe, po = banks[u]
+                nc.tensor.matmul_mx(out=acc[:], lhsT=wcodes[:, o, jb, wc].bitcast(FP8X4), lhsT_scale=wscl[:, o, jb, wc], rhs=xcodes[:, h, g, :].bitcast(FP8X4), rhs_scale=xscl[:, h, g, :], start=(g == 0), stop=(g == 1))
+        def pr(o, jb, h, k, c0=0, c1=512):
+            u = (o, jb, h)
+            if u not in prods:
+                prods[u] = {}
             ct, st = tabs[u]
-            if h == 0:
-                gp, gn = 1.0, -1.0
+            if h == 0: gp, gn = 1.0, -1.0
             else:
-                gp = gfac[:, 2 * o, jb : jb + 1]
-                gn = gfac[:, 2 * o + 1, jb : jb + 1]
-            ms = {}
-            for idx in range(4):
-                ms[idx] = work.tile([P, 512], F32, name="m%d" % idx, tag="m%d" % idx, bufs=3)
-            w = 512 // pieces
-            for piece in range(pieces):
-                cs = slice(w * piece, w * piece + w)
-                for idx, src, g, tab in ((0, pe, gp, ct), (3, pe, gp, st), (2, po, gp, ct), (1, po, gn, st)):
-                    if idx == 1 and ports is not None:
-                        ca = slice(0, 512 - 64)
-                        nc.vector.scalar_tensor_tensor(
-                            out=ms[idx][:, ca], in0=tab[:, ca], scalar=g, in1=src[:, ca], op0=ALU.mult, op1=ALU.mult
-                        )
-                        ports()
-                        cs = slice(512 - 64, 512)
-                    nc.vector.scalar_tensor_tensor(
-                        out=ms[idx][:, cs], in0=tab[:, cs], scalar=g, in1=src[:, cs], op0=ALU.mult, op1=ALU.mult
-                    )
-            prods[u] = ms
-
-        def pe_block(u_t, u_mx, t_first=False):
-            passes = mx_passes(u_mx) if u_mx is not None else []
-            last = u_t is not None and u_mx is None
-            ots = []
-            if u_t is not None:
-                ms = prods[u_t]
-                for b in range(2):
-                    ot = ps_o.tile([P, 2, 2, P], F32, name="ot", tag="ot")
-                    ots.append(ot)
-            for r in range(2):
-                if not t_first:
-                    for fn, c in passes[2 * r : 2 * r + 2]:
-                        fn(c)
-                if u_t is not None:
-                    if last:
-                        todo = [(r, s, e, z) for e in range(2) for s in range(2) for z in range(2)]
-                    else:
-                        todo = [(s, r, e, z) for e in range(2) for z in range(2) for s in range(2)]
-                    for b, qq, e, z in todo:
-                        q = 2 * b + qq
-                        nc.tensor.matmul(
-                            out=ots[b][:, qq, e, :], lhsT=ms[2 * e + z][:, P * q : P * q + P], rhs=ident[:],
-                            is_transpose=True, start=(z == 0), stop=(z == 1),
-                        )
-                if t_first:
-                    for fn, c in passes[2 * r : 2 * r + 2]:
-                        fn(c)
-            return ots
-
-        def evac(u, ots):
-            o, jb, h = u
-            for b in range(2):
-                sg = work.tile([P, 2, 256], F32, name="stg%d" % b, tag="stg%d" % b, bufs=3)
-                nc.scalar.copy(
-                    out=sg[:].rearrange("p q (j e) -> p q j e", e=2),
-                    in_=ots[b][:].rearrange("p q e j -> p q j e"),
-                )
-                t0 = 4 * h + 2 * b
-                nc.sync.dma_start(out=outs[o][:, t0 : t0 + 2, 256 * jb : 256 * jb + 256], in_=sg[:])
-
-        units = [(0, JB[0], 0), (1, JB[0], 0), (0, JB[0], 1), (1, JB[0], 1)]
-        units += [(o, jb, h) for jb in JB[1:] for o in range(2) for h in range(2)]
+                gp = gfac[:, 2 * o, jb : jb + 1]; gn = gfac[:, 2 * o + 1, jb : jb + 1]
+            idx, src, g, tb = ((0, 0, gp, ct), (3, 0, gp, st), (2, 1, gp, ct), (1, 1, gn, st))[k]
+            if idx not in prods[u]: prods[u][idx] = work.tile([P, 512], F32, name="m%d" % idx, tag="m%d" % idx, bufs=3)
+            cs = slice(c0, c1)
+            nc.vector.scalar_tensor_tensor(out=prods[u][idx][:, cs], in0=tb[:, cs], scalar=g, in1=banks[u][src][:, cs], op0=ALU.mult, op1=ALU.mult)
+        def tr(o, jb, h, b):
+            u = (o, jb, h); ms = prods[u]
+            ot = ps_o.tile([P, 2, 2, P], F32, name="ot", tag="ot")
+            otsd[(u, b)] = ot
+            for e in range(2):
+                for s in range(2):
+                    for z in range(2):
+                        q = 2 * b + s
+                        nc.tensor.matmul(out=ot[:, s, e, :], lhsT=ms[2 * e + z][:, P * q : P * q + P], rhs=ident[:], is_transpose=True, start=(z == 0), stop=(z == 1))
+        def ev(o, jb, h, b):
+            ot = otsd[((o, jb, h), b)]
+            sg = work.tile([P, 2, 256], F32, name="stg", tag="stg", bufs=6)
+            dst = sg[:].rearrange("p q (j e) -> p q j e", e=2); src = ot[:].rearrange("p q e j -> p q j e")
+            nc.scalar.copy(out=dst, in_=src)
+            t0 = 4 * h + 2 * b
+            nc.sync.dma_start(out=outs[o][:, t0 : t0 + 2, 256 * jb : 256 * jb + 256], in_=sg[:])
+        units = [(o, jb, h) for jb in JB for o in range(2) for h in range(2)]
         n_units = len(units)
 
-        def preps_s(n):
-            c, r = n // 4, n % 4
-            if c + 1 >= 4:
-                return
-            nxt = JB[c + 1]
-            if r == 0:
-                scdbl(nxt)
-                wil(0, nxt, 0)
-                wil(0, nxt, 1)
-            if r == 1:
-                trig_s(nxt)
-            if r == 2:
-                scdbl(4 + nxt)
-                wil(1, nxt, 0)
-            if r == 3:
-                wil(1, nxt, 1)
+        def xh(h, i):
+            xt(h, i)
+            xsc(h, i, 0)
+            xsc(h, i, 1)
 
-        def preps_v(n):
-            c, r = n // 4, n % 4
-            if r == 0 and 1 <= c < 4:
-                wquant(1, JB[c])
-            if r == 1 and c + 2 < 4:
-                rr_a(JB[c + 2])
-            if r == 2 and c + 1 < 4:
-                wquant(0, JB[c + 1])
-            if r == 3 and c + 2 < 4:
-                rr_b(JB[c + 2])
+        prep = []
+        for jb in JB[1:]:
+            prep += [
+                (dbl, (jb,)), (wil, (0, jb, 0)), (wil, (0, jb, 1)), (cos, (jb,)),
+                (sin, (jb,)), (dbl, (4 + jb,)), (wil, (1, jb, 0)), (wil, (1, jb, 1)),
+            ]
+        n_head = 9
+        n_spread = 10
 
-        def has_ports(n):
-            c, r = n // 4, n % 4
-            return (r == 0 and 1 <= c) or (r % 2 == 1 and c + 2 < 4) or (r == 2 and c + 1 < 4)
+        def prep_s(items):
+            for fn, a in items:
+                fn(*a)
 
-        rr_a(JB[0])
-        trig_s(JB[0])
-        scdbl(JB[0])
-        scdbl(4 + JB[0])
-        make_gfac()
-        rr_a(JB[1])
-        rr_b(JB[1])
-        wil(0, JB[0], 0, on_vector=True)
-        wil(0, JB[0], 1, on_vector=True)
-        wquant(0, JB[0])
-        xprep(0, 0)
-        xprep(0, 1)
-        prod(units[0], nc.vector)
-        prod(units[1], nc.vector)
-        xquant(0)
-        pe_block(None, units[0])
-        wil(1, JB[0], 0)
-        wil(1, JB[0], 1)
-        xprep(1, 0)
-        wquant(1, JB[0])
-        pe_block(None, units[1])
-        preps_s(0)
-        epi_v(units[0], 1, lambda: xprep(1, 1))
-        prod(units[2], nc.gpsimd)
-        ots = pe_block(units[0], None, t_first=True)
-        evac(units[0], ots)
-        preps_s(1)
-        epi_v(units[1], 1, lambda: xquant(1))
-        prod(units[3], nc.gpsimd)
-        ots = pe_block(units[1], units[2])
-        pe_block(None, units[3])
-        evac(units[1], ots)
-        preps_s(2)
-
-        def ports2():
-            preps_v(2)
-            preps_v(1)
-
-        epi_v(units[2], 1, ports2)
-        prod(units[4], nc.gpsimd)
-        for n in range(3, n_units + 1):
-            preps_s(n)
-            ots = pe_block(units[n - 1], units[n + 1] if n + 1 < n_units else None)
+        rra(JB[1])
+        wil(0, JB[0], 0, "v")
+        wil(0, JB[0], 1, "v")
+        rra(JB[2])
+        rrb(JB[1])
+        wil(1, JB[0], 0, "g")
+        wil(1, JB[0], 1, "g")
+        dbl(4 + JB[0])
+        for a in range(4):
+            cast(0, a)
+        xh(0, 0)
+        xh(0, 1)
+        sin(JB[0])
+        cast(1, 0)
+        dbl(JB[0])
+        for a in range(1, 4):
+            cast(1, a)
+        cos(JB[0])
+        for n in range(3):
+            tab(*units[n])
+        wq(0, JB[0])
+        xq(0)
+        wq(1, JB[0])
+        rra(JB[3])
+        xh(1, 0)
+        xh(1, 1)
+        xq(1)
+        gf()
+        mx(*units[0], 0)
+        mx(*units[0], 1)
+        prep_s(prep[:n_head])
+        rest = prep[n_head:]
+        for n in range(n_units + 1):
+            if n < n_units - 1:
+                for k in range(4):
+                    pr(*units[n], k)
+                if n == 0:
+                    rrb(JB[2])
+                if n == 4:
+                    rrb(JB[3])
+                if n % 2 == 1 and n + 3 < n_units:
+                    o, jb, h = units[n + 3]
+                    wq(o, jb)
+            if n == 0:
+                mx(*units[1], 0)
+                mx(*units[1], 1)
+            else:
+                for b in range(2):
+                    if n + 1 < n_units:
+                        mx(*units[n + 1], b)
+                    tr(*units[n - 1], b)
+                for b in range(2):
+                    ev(*units[n - 1], b)
+            if n < n_spread:
+                prep_s(rest[n * len(rest) // n_spread : (n + 1) * len(rest) // n_spread])
             if n == n_units - 1:
-                epi_v(units[n], 2)
-            elif n < n_units:
-                epi_v(units[n], 1, (lambda: preps_v(n)) if has_ports(n) else None)
-            if n + 2 < n_units:
-                prod(units[n + 2], nc.gpsimd)
-            evac(units[n - 1], ots)
+                for c in range(2):
+                    for k in range(4):
+                        pr(*units[n], k, 256 * c, 256 * c + 256)
+            if n + 3 < n_units:
+                tab(*units[n + 3])

@@ -117,11 +117,14 @@ def tile_simpleretention_pa_kernel(tc, X_bytes, X_scale, W_Q, W_K, out_0, out_1)
         xcodes = const.tile([P, 2, 2, 512], U32, name="xcodes", align_bytes=64)
         xscl = const.tile([P, 2, 2, 512], U8, name="xscl", align_bytes=64)
         xg = {}; xws = {}; xts = {}
-        def cast(h, a):
+        def cast(h, a, on_vector=False):
             xw = work.tile([P, KDIM], BF16, name="xw", tag="xw", bufs=4)
             xws[(h, a)] = xw
             src = xbytes[h][:, a, :].bitcast(FP8)
-            nc.scalar.copy(out=xw[:], in_=src)
+            if on_vector:
+                nc.vector.tensor_copy(out=xw[:], in_=src)
+            else:
+                nc.scalar.copy(out=xw[:], in_=src)
         def xt(h, i):
             xt = [ps_o.tile([P, 2, 256], F32, name="xt%d" % g, tag="ot") for g in range(2)]
             xts[(h, i)] = xt
@@ -213,7 +216,7 @@ def tile_simpleretention_pa_kernel(tc, X_bytes, X_scale, W_Q, W_K, out_0, out_1)
                 (dbl, (jb,)), (wil, (0, jb, 0)), (wil, (0, jb, 1)), (cos, (jb,)),
                 (sin, (jb,)), (dbl, (4 + jb,)), (wil, (1, jb, 0)), (wil, (1, jb, 1)),
             ]
-        n_head = 9
+        n_head = 8
         n_spread = 10
 
         def prep_s(items):
@@ -223,12 +226,11 @@ def tile_simpleretention_pa_kernel(tc, X_bytes, X_scale, W_Q, W_K, out_0, out_1)
         rra(JB[1])
         wil(0, JB[0], 0, "v")
         wil(0, JB[0], 1, "v")
-        rra(JB[2])
-        rrb(JB[1])
+        cast(0, 0, True)
         wil(1, JB[0], 0, "g")
         wil(1, JB[0], 1, "g")
         dbl(4 + JB[0])
-        for a in range(4):
+        for a in range(1, 4):
             cast(0, a)
         xh(0, 0)
         xh(0, 1)
@@ -243,6 +245,8 @@ def tile_simpleretention_pa_kernel(tc, X_bytes, X_scale, W_Q, W_K, out_0, out_1)
         wq(0, JB[0])
         xq(0)
         wq(1, JB[0])
+        rra(JB[2])
+        rrb(JB[1])
         rra(JB[3])
         xh(1, 0)
         xh(1, 1)
@@ -270,6 +274,7 @@ def tile_simpleretention_pa_kernel(tc, X_bytes, X_scale, W_Q, W_K, out_0, out_1)
                 for b in range(2):
                     if n + 1 < n_units:
                         mx(*units[n + 1], b)
+                for b in range(2):
                     tr(*units[n - 1], b)
                 for b in range(2):
                     ev(*units[n - 1], b)

@@ -42,11 +42,13 @@ def tile_simpleretention_pa_kernel(tc, X_bytes, X_scale, W_Q, W_K, out_0, out_1)
                 t = work.tile([P, 4, 256], BF16, name="wraw", tag="wraw", bufs=16)
                 wraw[(o, jb, g)] = t
                 nc.sync.dma_start(out=t[:], in_=weights[o][512 * g : 512 * (g + 1), 256 * jb : 256 * (jb + 1)].rearrange("(p t) n -> p t n", t=4))
-        load_w(0, JB[0])
         load_x(0)
+        load_w(0, JB[0])
         load_x(1)
+        load_w(0, JB[1])
+        load_w(1, JB[1])
         load_w(1, JB[0])
-        for jb in JB[1:]:
+        for jb in JB[2:]:
             load_w(0, jb)
             load_w(1, jb)
         ones = const.tile([P, 16], F32, name="ones")
@@ -93,6 +95,13 @@ def tile_simpleretention_pa_kernel(tc, X_bytes, X_scale, W_Q, W_K, out_0, out_1)
             for l in range(3):
                 w = 64 * 2**l
                 nc.scalar.activation(out=sc0[:, i, w : 2 * w], in_=sc0[:, i, 0:w], func=ACT.Copy, scale=pw[:, l, i : i + 1])
+        def dbl_v(l, pair):
+            w = 64 * 2**l
+            for i in pair:
+                nc.vector.tensor_scalar(
+                    out=sc0[:, i, w : 2 * w], in0=sc0[:, i, 0:w], scalar1=pw[:, l, i : i + 1], scalar2=None, op0=ALU.mult
+                )
+
         exps(0); exps(1); pws()
         trig = const.tile([P, 4, 2, TOK], F32, name="trig")
         kks = {}; nphs = {}; abss = {}
@@ -163,7 +172,7 @@ def tile_simpleretention_pa_kernel(tc, X_bytes, X_scale, W_Q, W_K, out_0, out_1)
             nc.vector.reciprocal(out=gfac[:, 2, :], in_=zcol[:])
             nc.vector.tensor_scalar(out=gfac[:, 3, :], in0=gfac[:, 2, :], scalar1=-1.0, scalar2=None, op0=ALU.mult)
         def tab(o, jb, h):
-            tb = work.tile([P, 2, 512], F32, name="tb", tag="tb", bufs=3)
+            tb = work.tile([P, 2, 512], F32, name="tb", tag="tb", bufs=2)
             nc.gpsimd.tensor_tensor(out=tb[:], in0=trig[:, jb, :, 512 * h : 512 * h + 512], in1=sc0[:, 4 * o + jb, :].unsqueeze(1).to_broadcast([P, 2, 512]), op=ALU.mult)
             tabs[(o, jb, h)] = (tb[:, 0, :], tb[:, 1, :])
         def mx(o, jb, h, e):
@@ -202,13 +211,9 @@ def tile_simpleretention_pa_kernel(tc, X_bytes, X_scale, W_Q, W_K, out_0, out_1)
             nc.scalar.copy(out=dst, in_=src)
             t0 = 4 * h + 2 * b
             nc.sync.dma_start(out=outs[o][:, t0 : t0 + 2, 256 * jb : 256 * jb + 256], in_=sg[:])
-        units = [(o, jb, h) for jb in JB for o in range(2) for h in range(2)]
+        units = [(o, JB[0], h) for h in range(2) for o in range(2)]
+        units += [(o, jb, h) for jb in JB[1:] for o in range(2) for h in range(2)]
         n_units = len(units)
-
-        def xh(h, i):
-            xt(h, i)
-            xsc(h, i, 0)
-            xsc(h, i, 1)
 
         prep = []
         for jb in JB[1:]:
@@ -216,56 +221,64 @@ def tile_simpleretention_pa_kernel(tc, X_bytes, X_scale, W_Q, W_K, out_0, out_1)
                 (dbl, (jb,)), (wil, (0, jb, 0)), (wil, (0, jb, 1)), (cos, (jb,)),
                 (sin, (jb,)), (dbl, (4 + jb,)), (wil, (1, jb, 0)), (wil, (1, jb, 1)),
             ]
-        n_head = 8
+        n_head = 7
         n_spread = 10
+        rest = prep[n_head:]
 
         def prep_s(items):
             for fn, a in items:
                 fn(*a)
 
-        rra(JB[1])
-        wil(0, JB[0], 0, "v")
-        wil(0, JB[0], 1, "v")
         cast(0, 0, True)
-        wil(1, JB[0], 0, "g")
-        wil(1, JB[0], 1, "g")
-        dbl(4 + JB[0])
+        dbl_v(0, (JB[0], 4 + JB[0]))
+        rra(JB[1])
+        dbl_v(1, (JB[0], 4 + JB[0]))
+        wil(0, JB[0], 0, "v")
+        dbl_v(2, (JB[0], 4 + JB[0]))
+        wil(0, JB[0], 1, "v")
+        rrb(JB[1])
         for a in range(1, 4):
             cast(0, a)
-        xh(0, 0)
-        xh(0, 1)
+        wil(1, JB[0], 0, "g")
+        wil(1, JB[0], 1, "g")
+        for i in range(2):
+            xt(0, i)
+            xsc(0, i, 0)
+            xsc(0, i, 1)
         sin(JB[0])
         cast(1, 0)
-        dbl(JB[0])
-        for a in range(1, 4):
-            cast(1, a)
+        cast(1, 1)
         cos(JB[0])
-        for n in range(3):
-            tab(*units[n])
+        tab(*units[0])
+        cast(1, 2)
+        cast(1, 3)
+        tab(*units[1])
         wq(0, JB[0])
         xq(0)
-        wq(1, JB[0])
-        rra(JB[2])
-        rrb(JB[1])
-        rra(JB[3])
-        xh(1, 0)
-        xh(1, 1)
-        xq(1)
-        gf()
+        xt(1, 0)
+        xt(1, 1)
         mx(*units[0], 0)
         mx(*units[0], 1)
+        gf()
+        for i in range(2):
+            xsc(1, i, 0)
+            xsc(1, i, 1)
+        wq(1, JB[0])
+        rra(JB[2])
+        rra(JB[3])
         prep_s(prep[:n_head])
-        rest = prep[n_head:]
         for n in range(n_units + 1):
             if n < n_units - 1:
                 for k in range(4):
                     pr(*units[n], k)
                 if n == 0:
+                    xq(1)
+                if n == 1:
                     rrb(JB[2])
-                if n == 4:
+                if n == 3:
                     rrb(JB[3])
-                if n % 2 == 1 and n + 3 < n_units:
-                    o, jb, h = units[n + 3]
+                if n >= 2 and n % 2 == 0 and n + 2 < n_units:
+                    o, jb, h = units[n + 2]
                     wq(o, jb)
             if n == 0:
                 mx(*units[1], 0)
@@ -284,5 +297,5 @@ def tile_simpleretention_pa_kernel(tc, X_bytes, X_scale, W_Q, W_K, out_0, out_1)
                 for c in range(2):
                     for k in range(4):
                         pr(*units[n], k, 256 * c, 256 * c + 256)
-            if n + 3 < n_units:
-                tab(*units[n + 3])
+            if n + 2 < n_units:
+                tab(*units[n + 2])

@@ -45,10 +45,8 @@ def tile_simpleretention_pa_kernel(tc, X_bytes, X_scale, W_Q, W_K, out_0, out_1)
         load_x(0)
         load_w(0, JB[0])
         load_x(1)
-        load_w(0, JB[1])
-        load_w(1, JB[1])
         load_w(1, JB[0])
-        for jb in JB[2:]:
+        for jb in JB[1:]:
             load_w(0, jb)
             load_w(1, jb)
         ones = const.tile([P, 16], F32, name="ones")

@@ -69,18 +69,23 @@ def tile_simpleretention_pa_kernel(tc, X_bytes, X_scale, W_Q, W_K, out_0, out_1)
             nc.vector.tensor_scalar(out=rrow[:, 16 * a : 16 * a + 16], in0=vv[:], scalar1=10000.0 ** (-16.0 * a / 512.0) / TWO_PI, scalar2=None, op0=ALU.mult)
         rt = ps_o.tile([P, 512], F32, name="rt", tag="ot")
         nc.tensor.transpose(rt[:, 0:P], rrow[:], ident[:])
+        fcol = const.tile([P, 4], F32, name="fcol")
+        nc.vector.tensor_copy(out=fcol[:, 0:1], in_=rt[:, 0:1])
         lsc = const.tile([P, 8], F32, name="lsc")
         nc.vector.tensor_scalar(out=lsc[:, 0:4], in0=lnz[:], scalar1=1.0 / 512.0, scalar2=None, op0=ALU.mult)
         nc.vector.tensor_scalar(out=lsc[:, 4:8], in0=lnz[:], scalar1=-1.0 / 512.0, scalar2=None, op0=ALU.mult)
         halfpi = const.tile([P, 1], F32, name="halfpi")
         nc.vector.tensor_scalar(out=halfpi[:], in0=ones[:, 0:1], scalar1=0.5 * math.pi, scalar2=None, op0=ALU.mult)
-        fcol = const.tile([P, 4], F32, name="fcol")
-        nc.vector.tensor_copy(out=fcol[:, 0:1], in_=rt[:, 0:1])
         ang3 = const.tile([P, 2], F32, name="ang3")
-        for jb in range(1, 4):
-            nc.vector.tensor_scalar(out=fcol[:, jb : jb + 1], in0=fcol[:, 0:1], scalar1=10000.0 ** (-128.0 * jb / 512.0), scalar2=None, op0=ALU.mult)
-        nc.vector.tensor_scalar(out=ang3[:, 0:1], in0=fcol[:, 3:4], scalar1=TWO_PI, scalar2=None, op0=ALU.mult)
-        nc.vector.tensor_scalar(out=ang3[:, 1:2], in0=fcol[:, 3:4], scalar1=-TWO_PI, scalar2=None, op0=ALU.mult)
+
+        def freqs():
+            for jb in range(1, 4):
+                nc.vector.tensor_scalar(
+                    out=fcol[:, jb : jb + 1], in0=fcol[:, 0:1], scalar1=10000.0 ** (-128.0 * jb / 512.0), scalar2=None, op0=ALU.mult
+                )
+            nc.vector.tensor_scalar(out=ang3[:, 0:1], in0=fcol[:, 3:4], scalar1=TWO_PI, scalar2=None, op0=ALU.mult)
+            nc.vector.tensor_scalar(out=ang3[:, 1:2], in0=fcol[:, 3:4], scalar1=-TWO_PI, scalar2=None, op0=ALU.mult)
+
         sc0 = const.tile([P, 8, 512], F32, name="sc0")
         pw = const.tile([P, 3, 8], F32, name="pw")
         def exps(part):
@@ -108,9 +113,45 @@ def tile_simpleretention_pa_kernel(tc, X_bytes, X_scale, W_Q, W_K, out_0, out_1)
             nc.vector.tensor_scalar(out=kk[:], in0=niota[:], scalar1=fcol[:, jb : jb + 1], scalar2=None, op0=ALU.mult)
             kks[jb] = kk
         def rrb(jb):
-            nph = work.tile([P, TOK], F32, name="nph", tag="nph", bufs=3)
+            nph = work.tile([P, TOK], F32, name="nph", tag="nph", bufs=2)
             nc.vector.scalar_tensor_tensor(out=nph[:], in0=niota[:], scalar=fcol[:, jb : jb + 1], in1=kks[jb][:], op0=ALU.mult, op1=ALU.subtract)
             nphs[jb] = nph
+        mid4 = const.tile([P, 4], F32, name="mid4")
+        nc.gpsimd.iota(mid4[:], pattern=[[512, 4]], base=255, channel_multiplier=0, allow_small_or_imprecise_dtypes=True)
+        m8 = const.tile([P, 2, 4], I32, name="m8")
+        q8 = const.tile([P, 2, 4], I32, name="q8")
+        r8 = const.tile([P, 2, 4], F32, name="r8")
+        s8 = const.tile([P, 2, 4], F32, name="s8")
+        t8 = const.tile([P, 2, 4], F32, name="t8")
+        b8 = const.tile([P, 2, 4], F32, name="b8")
+
+        def ht(k):
+            if k == 0:
+                nc.vector.tensor_scalar(out=m8[:, 0, :], in0=mid4[:], scalar1=fcol[:, 2:3], scalar2=None, op0=ALU.mult)
+                nc.vector.tensor_scalar(out=m8[:, 1, :], in0=mid4[:], scalar1=fcol[:, 2:3], scalar2=0.5, op0=ALU.mult, op1=ALU.add)
+            elif k == 1:
+                nc.vector.tensor_scalar(out=q8[:], in0=m8[:], scalar1=0.5, scalar2=None, op0=ALU.mult)
+            elif k == 2:
+                nc.vector.scalar_tensor_tensor(out=r8[:], in0=q8[:], scalar=-2.0, in1=m8[:], op0=ALU.mult, op1=ALU.add)
+            elif k == 3:
+                nc.vector.tensor_tensor(out=t8[:], in0=r8[:], in1=r8[:], op=ALU.mult)
+            elif k == 4:
+                nc.vector.tensor_scalar(out=s8[:], in0=t8[:], scalar1=-2.0, scalar2=1.0, op0=ALU.mult, op1=ALU.add)
+            elif k == 5:
+                nc.vector.scalar_tensor_tensor(out=b8[:], in0=m8[:], scalar=-math.pi, in1=s8[:], op0=ALU.mult, op1=ALU.mult)
+                nc.vector.tensor_scalar(out=t8[:], in0=s8[:], scalar1=fcol[:, 2:3], scalar2=TWO_PI, op0=ALU.mult, op1=ALU.mult)
+            else:
+                nc.vector.scalar_tensor_tensor(
+                    out=b8[:, 1, :], in0=s8[:, 1, :], scalar=0.5 * math.pi, in1=b8[:, 1, :], op0=ALU.mult, op1=ALU.add
+                )
+
+        def trig2(k):
+            for c in range(4):
+                cs = slice(256 * c, 256 * c + 256)
+                nc.scalar.activation(
+                    out=trig[:, 2, 1 - k, cs], in_=niota[:, cs], func=ACT.Sin, scale=t8[:, k, c : c + 1], bias=b8[:, k, c : c + 1]
+                )
+
         def sin(jb):
             if jb == 3: nc.scalar.activation(out=trig[:, jb, 1, :], in_=niota[:], func=ACT.Sin, scale=ang3[:, 0:1])
             else: nc.scalar.activation(out=trig[:, jb, 1, :], in_=nphs[jb][:], func=ACT.Sin, scale=TWO_PI)
@@ -152,7 +193,8 @@ def tile_simpleretention_pa_kernel(tc, X_bytes, X_scale, W_Q, W_K, out_0, out_1)
         wscl = const.tile([P, 2, 4, 512], U8, name="wscl", align_bytes=64)
         wgs = {}
         def wil(o, jb, g, e="s"):
-            if (o, jb) not in wgs: wgs[(o, jb)] = work.tile([P, 2, 2, P, 4], BF16, name="wg", tag="wg", bufs=3, align_bytes=64)
+            if (o, jb) not in wgs:
+                wgs[(o, jb)] = work.tile([P, 2, 2, P, 4], BF16, name="wg", tag="wg", bufs=3, align_bytes=64)
             wg = wgs[(o, jb)]
             src = wraw[(o, jb, g)][:].rearrange("p t (j e) -> p e j t", e=2)
             if e == "v": nc.vector.tensor_copy(out=wg[:, g, :, :, :], in_=src); return
@@ -160,6 +202,10 @@ def tile_simpleretention_pa_kernel(tc, X_bytes, X_scale, W_Q, W_K, out_0, out_1)
             src = wraw[(o, jb, g)][:].rearrange("p t (c i e) -> p e c t i", i=4, e=2)
             for ee in range(2):
                 nc.scalar.copy(out=wg[:, g, ee, :, :].rearrange("p (c i) t -> p c t i", i=4), in_=src[:, ee, :, :, :])
+        def hold_wg(o, jb):
+            wgs[(o, jb)] = work.tile([P, 2, 2, P, 4], BF16, name="wg", tag="wg", bufs=3, align_bytes=64)
+            nc.vector.memset(wgs[(o, jb)][:, 0, 0, 0, 0:2], 0.0)
+
         def wq(o, jb):
             nc.vector.quantize_mx(out=wcodes[:, o, jb, :].bitcast(FP8X4), scales=wscl[:, o, jb, :], in_=wgs[(o, jb)][:].rearrange("p g e j t -> p (g e j t)"))
         tabs = {}; banks = {}; prods = {}; otsd = {}
@@ -169,10 +215,23 @@ def tile_simpleretention_pa_kernel(tc, X_bytes, X_scale, W_Q, W_K, out_0, out_1)
             nc.vector.tensor_scalar(out=gfac[:, 1, :], in0=zcol[:], scalar1=-1.0, scalar2=None, op0=ALU.mult)
             nc.vector.reciprocal(out=gfac[:, 2, :], in_=zcol[:])
             nc.vector.tensor_scalar(out=gfac[:, 3, :], in0=gfac[:, 2, :], scalar1=-1.0, scalar2=None, op0=ALU.mult)
-        def tab(o, jb, h):
-            tb = work.tile([P, 2, 512], F32, name="tb", tag="tb", bufs=2)
-            nc.gpsimd.tensor_tensor(out=tb[:], in0=trig[:, jb, :, 512 * h : 512 * h + 512], in1=sc0[:, 4 * o + jb, :].unsqueeze(1).to_broadcast([P, 2, 512]), op=ALU.mult)
-            tabs[(o, jb, h)] = (tb[:, 0, :], tb[:, 1, :])
+        tbs = {}
+
+        def hold_tab(o, jb):
+            tbs[(o, jb)] = work.tile([P, 2, 2, 512], F32, name="tb", tag="tb", bufs=2)
+            nc.vector.memset(tbs[(o, jb)][:, 0, 0, 0:1], 0.0)
+
+        def tab(o, jb):
+            tb = tbs[(o, jb)]
+            nc.gpsimd.tensor_tensor(
+                out=tb[:].rearrange("p c h n -> p (c h) n"),
+                in0=trig[:, jb, :, :].rearrange("p c (h n) -> p (c h) n", h=2),
+                in1=sc0[:, 4 * o + jb, :].unsqueeze(1).to_broadcast([P, 4, 512]),
+                op=ALU.mult,
+            )
+            for h in range(2):
+                tabs[(o, jb, h)] = tb[:, :, h, :]
+
         def mx(o, jb, h, e):
             u = (o, jb, h)
             if u not in banks: banks[u] = {}
@@ -181,20 +240,29 @@ def tile_simpleretention_pa_kernel(tc, X_bytes, X_scale, W_Q, W_K, out_0, out_1)
             for g in range(2):
                 wc = slice(256 * g + P * e, 256 * g + P * e + P)
                 nc.tensor.matmul_mx(out=acc[:], lhsT=wcodes[:, o, jb, wc].bitcast(FP8X4), lhsT_scale=wscl[:, o, jb, wc], rhs=xcodes[:, h, g, :].bitcast(FP8X4), rhs_scale=xscl[:, h, g, :], start=(g == 0), stop=(g == 1))
-        def pr(o, jb, h, k, c0=0, c1=512):
-            u = (o, jb, h)
-            if u not in prods:
-                prods[u] = {}
-            ct, st = tabs[u]
-            if h == 0: gp, gn = 1.0, -1.0
+        def pr(u, c0=0, c1=512):
+            o, jb, h = u
+            tb = tabs[u]
+            pe, po = banks[u][0], banks[u][1]
+            if h == 0:
+                gp, gn = 1.0, -1.0
             else:
-                gp = gfac[:, 2 * o, jb : jb + 1]; gn = gfac[:, 2 * o + 1, jb : jb + 1]
-            idx, src, g, tb = ((0, 0, gp, ct), (3, 0, gp, st), (2, 1, gp, ct), (1, 1, gn, st))[k]
-            if idx not in prods[u]: prods[u][idx] = work.tile([P, 512], F32, name="m%d" % idx, tag="m%d" % idx, bufs=3)
+                gp = gfac[:, 2 * o, jb : jb + 1]
+                gn = gfac[:, 2 * o + 1, jb : jb + 1]
+            if c0 == 0:
+                prods[u] = [work.tile([P, 2, 512], F32, name="m%d" % e, tag="m%d" % e, bufs=3) for e in range(2)]
+            me, mo = prods[u]
             cs = slice(c0, c1)
-            nc.vector.scalar_tensor_tensor(out=prods[u][idx][:, cs], in0=tb[:, cs], scalar=g, in1=banks[u][src][:, cs], op0=ALU.mult, op1=ALU.mult)
+            nc.vector.scalar_tensor_tensor(
+                out=me[:, :, cs], in0=tb[:, :, cs], scalar=gp, in1=pe[:, cs].unsqueeze(1).to_broadcast([P, 2, c1 - c0]), op0=ALU.mult, op1=ALU.mult
+            )
+            nc.vector.scalar_tensor_tensor(out=mo[:, 0, cs], in0=tb[:, 0, cs], scalar=gp, in1=po[:, cs], op0=ALU.mult, op1=ALU.mult)
+            nc.vector.scalar_tensor_tensor(out=mo[:, 1, cs], in0=tb[:, 1, cs], scalar=gn, in1=po[:, cs], op0=ALU.mult, op1=ALU.mult)
+
         def tr(o, jb, h, b):
-            u = (o, jb, h); ms = prods[u]
+            u = (o, jb, h)
+            me, mo = prods[u]
+            ms = (me[:, 0, :], mo[:, 1, :], mo[:, 0, :], me[:, 1, :])
             ot = ps_o.tile([P, 2, 2, P], F32, name="ot", tag="ot")
             otsd[(u, b)] = ot
             for e in range(2):
@@ -209,17 +277,18 @@ def tile_simpleretention_pa_kernel(tc, X_bytes, X_scale, W_Q, W_K, out_0, out_1)
             nc.scalar.copy(out=dst, in_=src)
             t0 = 4 * h + 2 * b
             nc.sync.dma_start(out=outs[o][:, t0 : t0 + 2, 256 * jb : 256 * jb + 256], in_=sg[:])
-        units = [(o, JB[0], h) for h in range(2) for o in range(2)]
-        units += [(o, jb, h) for jb in JB[1:] for o in range(2) for h in range(2)]
+        units = [(o, jb, h) for jb in JB for o in range(2) for h in range(2)]
         n_units = len(units)
 
         prep = []
         for jb in JB[1:]:
-            prep += [
-                (dbl, (jb,)), (wil, (0, jb, 0)), (wil, (0, jb, 1)), (cos, (jb,)),
-                (sin, (jb,)), (dbl, (4 + jb,)), (wil, (1, jb, 0)), (wil, (1, jb, 1)),
-            ]
-        n_head = 7
+            if jb == 2:
+                waves = [(trig2, (1,)), (trig2, (0,))]
+            else:
+                waves = [(cos, (jb,)), (sin, (jb,))]
+            prep += [(dbl, (jb,)), (wil, (0, jb, 0)), (wil, (0, jb, 1))] + waves
+            prep += [(dbl, (4 + jb,)), (wil, (1, jb, 0)), (wil, (1, jb, 1))]
+        n_head = 9
         n_spread = 10
         rest = prep[n_head:]
 
@@ -227,16 +296,27 @@ def tile_simpleretention_pa_kernel(tc, X_bytes, X_scale, W_Q, W_K, out_0, out_1)
             for fn, a in items:
                 fn(*a)
 
-        cast(0, 0, True)
-        dbl_v(0, (JB[0], 4 + JB[0]))
+        first = (JB[0], 4 + JB[0])
         rra(JB[1])
-        dbl_v(1, (JB[0], 4 + JB[0]))
+        freqs()
+        cast(0, 0, True)
+        ht(0)
+        dbl_v(0, first)
+        ht(1)
         wil(0, JB[0], 0, "v")
-        dbl_v(2, (JB[0], 4 + JB[0]))
+        ht(2)
+        dbl_v(1, first)
+        ht(3)
         wil(0, JB[0], 1, "v")
+        ht(4)
+        dbl_v(2, first)
+        ht(5)
+        rra(JB[2])
+        ht(6)
         rrb(JB[1])
         for a in range(1, 4):
             cast(0, a)
+        hold_wg(1, JB[0])
         wil(1, JB[0], 0, "g")
         wil(1, JB[0], 1, "g")
         for i in range(2):
@@ -247,12 +327,12 @@ def tile_simpleretention_pa_kernel(tc, X_bytes, X_scale, W_Q, W_K, out_0, out_1)
         cast(1, 0)
         cast(1, 1)
         cos(JB[0])
-        tab(*units[0])
         cast(1, 2)
         cast(1, 3)
-        tab(*units[1])
         wq(0, JB[0])
         xq(0)
+        hold_tab(0, JB[0])
+        tab(0, JB[0])
         xt(1, 0)
         xt(1, 1)
         mx(*units[0], 0)
@@ -261,27 +341,23 @@ def tile_simpleretention_pa_kernel(tc, X_bytes, X_scale, W_Q, W_K, out_0, out_1)
         for i in range(2):
             xsc(1, i, 0)
             xsc(1, i, 1)
+        xq(1)
+        mx(*units[1], 0)
+        mx(*units[1], 1)
         wq(1, JB[0])
-        rra(JB[2])
-        rra(JB[3])
+        rrb(JB[2])
+        hold_tab(1, JB[0])
+        tab(1, JB[0])
         prep_s(prep[:n_head])
         for n in range(n_units + 1):
+            pair_ends = n % 2 == 1 and n + 3 < n_units
             if n < n_units - 1:
-                for k in range(4):
-                    pr(*units[n], k)
-                if n == 0:
-                    xq(1)
-                if n == 1:
-                    rrb(JB[2])
-                if n == 3:
-                    rrb(JB[3])
-                if n >= 2 and n % 2 == 0 and n + 2 < n_units:
-                    o, jb, h = units[n + 2]
+                pr(units[n])
+                if pair_ends:
+                    o, jb, h = units[n + 3]
                     wq(o, jb)
-            if n == 0:
-                mx(*units[1], 0)
-                mx(*units[1], 1)
-            else:
+                    hold_tab(o, jb)
+            if n > 0:
                 for b in range(2):
                     if n + 1 < n_units:
                         mx(*units[n + 1], b)
@@ -293,7 +369,7 @@ def tile_simpleretention_pa_kernel(tc, X_bytes, X_scale, W_Q, W_K, out_0, out_1)
                 prep_s(rest[n * len(rest) // n_spread : (n + 1) * len(rest) // n_spread])
             if n == n_units - 1:
                 for c in range(2):
-                    for k in range(4):
-                        pr(*units[n], k, 256 * c, 256 * c + 256)
-            if n + 2 < n_units:
-                tab(*units[n + 2])
+                    pr(units[n], 256 * c, 256 * c + 256)
+            if pair_ends:
+                o, jb, h = units[n + 3]
+                tab(o, jb)

@@ -98,11 +98,17 @@ def tile_simpleretention_pa_kernel(tc, X_bytes, X_scale, W_Q, W_K, out_0, out_1)
             for l in range(3):
                 w = 64 * 2**l
                 nc.scalar.activation(out=sc0[:, i, w : 2 * w], in_=sc0[:, i, 0:w], func=ACT.Copy, scale=pw[:, l, i : i + 1])
-        def dbl_v(l, pair):
+        def dbl_v(l, i):
             w = 64 * 2**l
-            for i in pair:
-                nc.vector.tensor_scalar(
-                    out=sc0[:, i, w : 2 * w], in0=sc0[:, i, 0:w], scalar1=pw[:, l, i : i + 1], scalar2=None, op0=ALU.mult
+            nc.vector.tensor_scalar(
+                out=sc0[:, i, w : 2 * w], in0=sc0[:, i, 0:w], scalar1=pw[:, l, i : i + 1], scalar2=None, op0=ALU.mult
+            )
+
+        def dbl_g(i):
+            for l in range(3):
+                w = 64 * 2**l
+                nc.gpsimd.tensor_scalar(
+                    out=sc0[:, i, w : 2 * w], in0=sc0[:, i, 0:w], scalar1=pw[:, l, i : i + 1], scalar2=0.0, op0=ALU.mult, op1=ALU.add
                 )
 
         exps(0); exps(1); pws()
@@ -111,6 +117,14 @@ def tile_simpleretention_pa_kernel(tc, X_bytes, X_scale, W_Q, W_K, out_0, out_1)
         def rra(jb):
             kk = work.tile([P, TOK], I32, name="kk", tag="kk", bufs=2)
             nc.vector.tensor_scalar(out=kk[:], in0=niota[:], scalar1=fcol[:, jb : jb + 1], scalar2=None, op0=ALU.mult)
+            kks[jb] = kk
+
+        def rra_g(jb):
+            kk = work.tile([P, TOK], I32, name="kk", tag="kk", bufs=2)
+            nc.vector.memset(kk[:, 0:1], 0)
+            nc.gpsimd.tensor_scalar(
+                out=kk[:], in0=niota[:], scalar1=fcol[:, jb : jb + 1], scalar2=0.0, op0=ALU.mult, op1=ALU.add
+            )
             kks[jb] = kk
         def rrb(jb):
             nph = work.tile([P, TOK], F32, name="nph", tag="nph", bufs=2)
@@ -189,6 +203,22 @@ def tile_simpleretention_pa_kernel(tc, X_bytes, X_scale, W_Q, W_K, out_0, out_1)
                 in1=xs[:, g, :].rearrange("p (u e) -> p u e", e=2).unsqueeze(1).to_broadcast([P, 256, 2, 2]), op=ALU.mult)
         def xq(h):
             nc.vector.quantize_mx(out=xcodes[:, h, :, :].rearrange("p g r -> p (g r)").bitcast(FP8X4), scales=xscl[:, h, :, :].rearrange("p g r -> p (g r)"), in_=xg[h][:].rearrange("p g r t -> p (g r t)"))
+        identb = const.tile([P, P], BF16, name="identb")
+        nc.vector.tensor_copy(out=identb[:], in_=ident[:])
+        wps = {}
+
+        def wpe(o, jb, g, k):
+            ps = ps_p.tile([P, 2, P, 4], BF16, name="wps", tag="acc%d" % k)
+            wps[(o, jb, g)] = ps
+            src = wraw[(o, jb, g)][:].rearrange("p t (j e) -> p e j t", e=2)
+            for e in range(2):
+                nc.tensor.matmul(out=ps[:, e, :, :], lhsT=identb[:], rhs=src[:, e, :, :], start=True, stop=True)
+
+        def wout(o, jb, g):
+            if (o, jb) not in wgs:
+                wgs[(o, jb)] = work.tile([P, 2, 2, P, 4], BF16, name="wg", tag="wg", bufs=3, align_bytes=64)
+            nc.vector.tensor_copy(out=wgs[(o, jb)][:, g, :, :, :], in_=wps[(o, jb, g)][:])
+
         wcodes = const.tile([P, 2, 4, 512], U32, name="wcodes", align_bytes=64)
         wscl = const.tile([P, 2, 4, 512], U8, name="wscl", align_bytes=64)
         wgs = {}
@@ -198,14 +228,9 @@ def tile_simpleretention_pa_kernel(tc, X_bytes, X_scale, W_Q, W_K, out_0, out_1)
             wg = wgs[(o, jb)]
             src = wraw[(o, jb, g)][:].rearrange("p t (j e) -> p e j t", e=2)
             if e == "v": nc.vector.tensor_copy(out=wg[:, g, :, :, :], in_=src); return
-            if e == "g": nc.gpsimd.tensor_scalar(out=wg[:, g, :, :, :], in0=src, scalar1=1.0, scalar2=0.0, op0=ALU.mult, op1=ALU.add); return
             src = wraw[(o, jb, g)][:].rearrange("p t (c i e) -> p e c t i", i=4, e=2)
             for ee in range(2):
                 nc.scalar.copy(out=wg[:, g, ee, :, :].rearrange("p (c i) t -> p c t i", i=4), in_=src[:, ee, :, :, :])
-        def hold_wg(o, jb):
-            wgs[(o, jb)] = work.tile([P, 2, 2, P, 4], BF16, name="wg", tag="wg", bufs=3, align_bytes=64)
-            nc.vector.memset(wgs[(o, jb)][:, 0, 0, 0, 0:2], 0.0)
-
         def wq(o, jb):
             nc.vector.quantize_mx(out=wcodes[:, o, jb, :].bitcast(FP8X4), scales=wscl[:, o, jb, :], in_=wgs[(o, jb)][:].rearrange("p g e j t -> p (g e j t)"))
         tabs = {}; banks = {}; prods = {}; otsd = {}
@@ -286,9 +311,11 @@ def tile_simpleretention_pa_kernel(tc, X_bytes, X_scale, W_Q, W_K, out_0, out_1)
                 waves = [(trig2, (1,)), (trig2, (0,))]
             else:
                 waves = [(cos, (jb,)), (sin, (jb,))]
-            prep += [(dbl, (jb,)), (wil, (0, jb, 0)), (wil, (0, jb, 1))] + waves
+            if jb != JB[1]:
+                prep += [(dbl, (jb,))]
+            prep += [(wil, (0, jb, 0)), (wil, (0, jb, 1))] + waves
             prep += [(dbl, (4 + jb,)), (wil, (1, jb, 0)), (wil, (1, jb, 1))]
-        n_head = 9
+        n_head = 8
         n_spread = 10
         rest = prep[n_head:]
 
@@ -296,33 +323,37 @@ def tile_simpleretention_pa_kernel(tc, X_bytes, X_scale, W_Q, W_K, out_0, out_1)
             for fn, a in items:
                 fn(*a)
 
-        first = (JB[0], 4 + JB[0])
         rra(JB[1])
         freqs()
         cast(0, 0, True)
         ht(0)
-        dbl_v(0, first)
+        dbl_v(0, JB[0])
         ht(1)
         wil(0, JB[0], 0, "v")
         ht(2)
-        dbl_v(1, first)
+        dbl_v(1, JB[0])
         ht(3)
         wil(0, JB[0], 1, "v")
         ht(4)
-        dbl_v(2, first)
+        dbl_v(2, JB[0])
         ht(5)
-        rra(JB[2])
         ht(6)
         rrb(JB[1])
         for a in range(1, 4):
             cast(0, a)
-        hold_wg(1, JB[0])
-        wil(1, JB[0], 0, "g")
-        wil(1, JB[0], 1, "g")
-        for i in range(2):
-            xt(0, i)
-            xsc(0, i, 0)
-            xsc(0, i, 1)
+        rra_g(JB[2])
+        dbl_g(4 + JB[0])
+        dbl_g(JB[1])
+        xt(0, 0)
+        wpe(1, JB[0], 0, 0)
+        xsc(0, 0, 0)
+        xsc(0, 0, 1)
+        xt(0, 1)
+        wpe(1, JB[0], 1, 1)
+        xsc(0, 1, 0)
+        wout(1, JB[0], 0)
+        xsc(0, 1, 1)
+        wout(1, JB[0], 1)
         sin(JB[0])
         cast(1, 0)
         cast(1, 1)
@@ -345,7 +376,6 @@ def tile_simpleretention_pa_kernel(tc, X_bytes, X_scale, W_Q, W_K, out_0, out_1)
         mx(*units[1], 0)
         mx(*units[1], 1)
         wq(1, JB[0])
-        rrb(JB[2])
         hold_tab(1, JB[0])
         tab(1, JB[0])
         prep_s(prep[:n_head])
@@ -356,13 +386,17 @@ def tile_simpleretention_pa_kernel(tc, X_bytes, X_scale, W_Q, W_K, out_0, out_1)
                 if pair_ends:
                     o, jb, h = units[n + 3]
                     wq(o, jb)
+                    if n == 1:
+                        rrb(JB[2])
                     hold_tab(o, jb)
             if n > 0:
-                for b in range(2):
-                    if n + 1 < n_units:
-                        mx(*units[n + 1], b)
-                for b in range(2):
-                    tr(*units[n - 1], b)
+                steps = [(mx, n + 1), (tr, n - 1)]
+                if n % 2 == 0:
+                    steps = [steps[1], steps[0]]
+                for fn, k in steps:
+                    for b in range(2):
+                        if k < n_units:
+                            fn(*units[k], b)
                 for b in range(2):
                     ev(*units[n - 1], b)
             if n < n_spread:

@@ -83,6 +83,8 @@ def tile_simpleretention_pa_kernel(tc, X_bytes, X_scale, W_Q, W_K, out_0, out_1)
                 nc.vector.tensor_scalar(
                     out=fcol[:, jb : jb + 1], in0=fcol[:, 0:1], scalar1=10000.0 ** (-128.0 * jb / 512.0), scalar2=None, op0=ALU.mult
                 )
+
+        def rads():
             nc.vector.tensor_scalar(out=ang3[:, 0:1], in0=fcol[:, 3:4], scalar1=TWO_PI, scalar2=None, op0=ALU.mult)
             nc.vector.tensor_scalar(out=ang3[:, 1:2], in0=fcol[:, 3:4], scalar1=-TWO_PI, scalar2=None, op0=ALU.mult)
 
@@ -228,9 +230,10 @@ def tile_simpleretention_pa_kernel(tc, X_bytes, X_scale, W_Q, W_K, out_0, out_1)
             wg = wgs[(o, jb)]
             src = wraw[(o, jb, g)][:].rearrange("p t (j e) -> p e j t", e=2)
             if e == "v": nc.vector.tensor_copy(out=wg[:, g, :, :, :], in_=src); return
-            src = wraw[(o, jb, g)][:].rearrange("p t (c i e) -> p e c t i", i=4, e=2)
-            for ee in range(2):
-                nc.scalar.copy(out=wg[:, g, ee, :, :].rearrange("p (c i) t -> p c t i", i=4), in_=src[:, ee, :, :, :])
+            nc.scalar.copy(
+                out=wg[:, g, :, :, :].rearrange("p e (c i) t -> p c t e i", i=4),
+                in_=wraw[(o, jb, g)][:].rearrange("p t (c i e) -> p c t e i", i=4, e=2),
+            )
         def wq(o, jb):
             nc.vector.quantize_mx(out=wcodes[:, o, jb, :].bitcast(FP8X4), scales=wscl[:, o, jb, :], in_=wgs[(o, jb)][:].rearrange("p g e j t -> p (g e j t)"))
         tabs = {}; banks = {}; prods = {}; otsd = {}
@@ -284,24 +287,27 @@ def tile_simpleretention_pa_kernel(tc, X_bytes, X_scale, W_Q, W_K, out_0, out_1)
             nc.vector.scalar_tensor_tensor(out=mo[:, 0, cs], in0=tb[:, 0, cs], scalar=gp, in1=po[:, cs], op0=ALU.mult, op1=ALU.mult)
             nc.vector.scalar_tensor_tensor(out=mo[:, 1, cs], in0=tb[:, 1, cs], scalar=gn, in1=po[:, cs], op0=ALU.mult, op1=ALU.mult)
 
-        def tr(o, jb, h, b):
+        def tr(o, jb, h, q0, nq=2):
             u = (o, jb, h)
             me, mo = prods[u]
             ms = (me[:, 0, :], mo[:, 1, :], mo[:, 0, :], me[:, 1, :])
-            ot = ps_o.tile([P, 2, 2, P], F32, name="ot", tag="ot")
-            otsd[(u, b)] = ot
+            ot = ps_o.tile([P, nq, 2, P], F32, name="ot", tag="ot")
+            otsd[(u, q0)] = ot
             for e in range(2):
-                for s in range(2):
+                for s in range(nq):
                     for z in range(2):
-                        q = 2 * b + s
-                        nc.tensor.matmul(out=ot[:, s, e, :], lhsT=ms[2 * e + z][:, P * q : P * q + P], rhs=ident[:], is_transpose=True, start=(z == 0), stop=(z == 1))
-        def ev(o, jb, h, b):
-            ot = otsd[((o, jb, h), b)]
+                        ts = slice(P * (q0 + s), P * (q0 + s) + P)
+                        nc.tensor.matmul(
+                            out=ot[:, s, e, :], lhsT=ms[2 * e + z][:, ts], rhs=ident[:], is_transpose=True, start=(z == 0), stop=(z == 1)
+                        )
+
+        def ev(o, jb, h, q0, nq=2, copy=nc.scalar.copy):
+            ot = otsd[((o, jb, h), q0)]
             sg = work.tile([P, 2, 256], F32, name="stg", tag="stg", bufs=6)
-            dst = sg[:].rearrange("p q (j e) -> p q j e", e=2); src = ot[:].rearrange("p q e j -> p q j e")
-            nc.scalar.copy(out=dst, in_=src)
-            t0 = 4 * h + 2 * b
-            nc.sync.dma_start(out=outs[o][:, t0 : t0 + 2, 256 * jb : 256 * jb + 256], in_=sg[:])
+            copy(out=sg[:, 0:nq, :].rearrange("p q (j e) -> p q j e", e=2), in_=ot[:].rearrange("p q e j -> p q j e"))
+            t0 = 4 * h + q0
+            nc.sync.dma_start(out=outs[o][:, t0 : t0 + nq, 256 * jb : 256 * jb + 256], in_=sg[:, 0:nq, :])
+
         units = [(o, jb, h) for jb in JB for o in range(2) for h in range(2)]
         n_units = len(units)
 
@@ -325,6 +331,8 @@ def tile_simpleretention_pa_kernel(tc, X_bytes, X_scale, W_Q, W_K, out_0, out_1)
 
         rra(JB[1])
         freqs()
+        gf()
+        rads()
         cast(0, 0, True)
         ht(0)
         dbl_v(0, JB[0])
@@ -368,7 +376,6 @@ def tile_simpleretention_pa_kernel(tc, X_bytes, X_scale, W_Q, W_K, out_0, out_1)
         xt(1, 1)
         mx(*units[0], 0)
         mx(*units[0], 1)
-        gf()
         for i in range(2):
             xsc(1, i, 0)
             xsc(1, i, 1)
@@ -390,20 +397,24 @@ def tile_simpleretention_pa_kernel(tc, X_bytes, X_scale, W_Q, W_K, out_0, out_1)
                         rrb(JB[2])
                     hold_tab(o, jb)
             if n > 0:
-                steps = [(mx, n + 1), (tr, n - 1)]
+                last = n == n_units
+                parts = ((0, 2), (2, 1), (3, 1)) if last else ((0, 2), (2, 2))
                 if n % 2 == 0:
-                    steps = [steps[1], steps[0]]
-                for fn, k in steps:
-                    for b in range(2):
-                        if k < n_units:
-                            fn(*units[k], b)
-                for b in range(2):
-                    ev(*units[n - 1], b)
+                    for q0, nq in parts:
+                        tr(*units[n - 1], q0, nq)
+                for e in range(2):
+                    if n + 1 < n_units:
+                        mx(*units[n + 1], e)
+                if n % 2 == 1:
+                    for q0, nq in parts:
+                        tr(*units[n - 1], q0, nq)
+                for q0, nq in parts:
+                    ev(*units[n - 1], q0, nq, nc.vector.tensor_copy if last and q0 == 2 else nc.scalar.copy)
             if n < n_spread:
                 prep_s(rest[n * len(rest) // n_spread : (n + 1) * len(rest) // n_spread])
             if n == n_units - 1:
-                for c in range(2):
-                    pr(units[n], 256 * c, 256 * c + 256)
+                for c0, c1 in ((0, 256), (256, 384), (384, 512)):
+                    pr(units[n], c0, c1)
             if pair_ends:
                 o, jb, h = units[n + 3]
                 tab(o, jb)

from contextlib import ExitStack
import math
import concourse.mybir as mybir
from concourse.masks import make_identity
F32 = mybir.dt.float32
BF16 = mybir.dt.bfloat16
U8 = mybir.dt.uint8
U32 = mybir.dt.uint32
I32 = mybir.dt.int32
FP8 = mybir.dt.float8_e4m3fn
FP8X4 = mybir.dt.float8_e4m3fn_x4
ALU = mybir.AluOpType
ACT = mybir.ActivationFunctionType
P = 128
TOK = 1024
KDIM = 1024
TWO_PI = 2.0 * math.pi
CH = 1024
FLOPS = 2 * TOK * KDIM * 2 * CH
JB = (3, 0, 1, 2)


def tile_simpleretention_pa_kernel(tc, X_bytes, X_scale, W_Q, W_K, out_0, out_1):
    nc = tc.nc
    weights = (W_Q, W_K)
    outs = (out_0.rearrange("b (t p) c -> p (b t) c", p=P), out_1.rearrange("b (t p) c -> p (b t) c", p=P))
    xb_view = X_bytes.rearrange("b (a p) k -> p (b a) k", p=P)
    with ExitStack() as ctx:
        const = ctx.enter_context(tc.tile_pool(name="const", bufs=1))
        work = ctx.enter_context(tc.tile_pool(name="work", bufs=2))
        ps_p = ctx.enter_context(tc.psum_pool(name="psp", bufs=2))
        ps_o = ctx.enter_context(tc.psum_pool(name="pso", bufs=4))
        ctx.enter_context(tc.manual_schedule())
        xs = const.tile([P, 2, 4], F32, name="xs")
        nc.scalar.dma_start(out=xs[:], in_=X_scale.rearrange("a b (g p t) -> p (a b g) t", p=P, t=4))
        xbytes = [const.tile([P, 4, KDIM], U8, name="xbytes%d" % h) for h in range(2)]
        wraw = {}
        def load_x(h):
            nc.sync.dma_start(out=xbytes[h][:], in_=xb_view[:, 4 * h : 4 * h + 4, :])
        def load_w(o, jb):
            for g in range(2):
                t = work.tile([P, 4, 256], BF16, name="wraw", tag="wraw", bufs=16)
                wraw[(o, jb, g)] = t
                nc.sync.dma_start(out=t[:], in_=weights[o][512 * g : 512 * (g + 1), 256 * jb : 256 * (jb + 1)].rearrange("(p t) n -> p t n", t=4))
        load_x(0)
        load_w(0, JB[0])
        load_x(1)
        load_w(1, JB[0])
        for jb in JB[1:]:
            load_w(0, jb)
            load_w(1, jb)
        ones = const.tile([P, 16], F32, name="ones")
        nc.vector.memset(ones[:], 1.0)
        jcol = const.tile([P, 4], F32, name="jcol")
        nc.gpsimd.iota(jcol[:], pattern=[[P, 4]], base=0, channel_multiplier=1, allow_small_or_imprecise_dtypes=True)
        ident = const.tile([P, P], F32, name="ident")
        make_identity(nc, ident[:])
        niota = const.tile([P, TOK], F32, name="niota")
        nc.gpsimd.iota(niota[:], pattern=[[1, TOK]], base=0, channel_multiplier=0, allow_small_or_imprecise_dtypes=True)
        zcol = const.tile([P, 4], F32, name="zcol")
        nc.vector.tensor_scalar(out=zcol[:], in0=jcol[:], scalar1=2.0 / (1.4 * 1024), scalar2=(0.4 * 1024) / (1.4 * 1024), op0=ALU.mult, op1=ALU.add)
        lnz = const.tile([P, 4], F32, name="lnz")
        nc.scalar.activation(out=lnz[:], in_=zcol[:], func=ACT.Ln)
        vv = const.tile([P, 16], F32, name="vv")
        for b in range(16):
            nc.vector.tensor_scalar(out=vv[:, b : b + 1], in0=ones[:, b : b + 1], scalar1=10000.0 ** (-b / 512.0), scalar2=None, op0=ALU.mult)
        rrow = const.tile([P, P], F32, name="rrow")
        for a in range(8):
            nc.vector.tensor_scalar(out=rrow[:, 16 * a : 16 * a + 16], in0=vv[:], scalar1=10000.0 ** (-16.0 * a / 512.0) / TWO_PI, scalar2=None, op0=ALU.mult)
        rt = ps_o.tile([P, 512], F32, name="rt", tag="ot")
        nc.tensor.transpose(rt[:, 0:P], rrow[:], ident[:])
        fcol = const.tile([P, 4], F32, name="fcol")
        nc.vector.tensor_copy(out=fcol[:, 0:1], in_=rt[:, 0:1])
        lsc = const.tile([P, 8], F32, name="lsc")
        nc.vector.tensor_scalar(out=lsc[:, 0:4], in0=lnz[:], scalar1=1.0 / 512.0, scalar2=None, op0=ALU.mult)
        nc.vector.tensor_scalar(out=lsc[:, 4:8], in0=lnz[:], scalar1=-1.0 / 512.0, scalar2=None, op0=ALU.mult)
        halfpi = const.tile([P, 1], F32, name="halfpi")
        nc.vector.tensor_scalar(out=halfpi[:], in0=ones[:, 0:1], scalar1=0.5 * math.pi, scalar2=None, op0=ALU.mult)
        ang3 = const.tile([P, 2], F32, name="ang3")

        def freqs():
            for jb in range(1, 4):
                nc.vector.tensor_scalar(
                    out=fcol[:, jb : jb + 1], in0=fcol[:, 0:1], scalar1=10000.0 ** (-128.0 * jb / 512.0), scalar2=None, op0=ALU.mult
                )

        def rads():
            nc.vector.tensor_scalar(out=ang3[:, 0:1], in0=fcol[:, 3:4], scalar1=TWO_PI, scalar2=None, op0=ALU.mult)
            nc.vector.tensor_scalar(out=ang3[:, 1:2], in0=fcol[:, 3:4], scalar1=-TWO_PI, scalar2=None, op0=ALU.mult)

        sc0 = const.tile([P, 8, 512], F32, name="sc0")
        pw = const.tile([P, 3, 8], F32, name="pw")
        def exps(part):
            for i in ((3, 7) if part == 0 else (0, 4, 1, 5, 2, 6)):
                nc.scalar.activation(out=sc0[:, i, 0:64], in_=niota[:, 0:64], func=ACT.Exp, scale=lsc[:, i : i + 1])
        def pws():
            for l in range(3):
                nc.scalar.activation(out=pw[:, l, :], in_=lsc[:], func=ACT.Exp, scale=64.0 * 2**l)
        def dbl(i):
            for l in range(3):
                w = 64 * 2**l
                nc.scalar.activation(out=sc0[:, i, w : 2 * w], in_=sc0[:, i, 0:w], func=ACT.Copy, scale=pw[:, l, i : i + 1])
        def dbl_v(l, i):
            w = 64 * 2**l
            nc.vector.tensor_scalar(
                out=sc0[:, i, w : 2 * w], in0=sc0[:, i, 0:w], scalar1=pw[:, l, i : i + 1], scalar2=None, op0=ALU.mult
            )

        def dbl_g(i):
            for l in range(3):
                w = 64 * 2**l
                nc.gpsimd.tensor_scalar(
                    out=sc0[:, i, w : 2 * w], in0=sc0[:, i, 0:w], scalar1=pw[:, l, i : i + 1], scalar2=0.0, op0=ALU.mult, op1=ALU.add
                )

        exps(0); exps(1); pws()
        trig = const.tile([P, 4, 2, TOK], F32, name="trig")
        kks = {}; nphs = {}; abss = {}
        def rra(jb):
            kk = work.tile([P, TOK], I32, name="kk", tag="kk", bufs=2)
            nc.vector.tensor_scalar(out=kk[:], in0=niota[:], scalar1=fcol[:, jb : jb + 1], scalar2=None, op0=ALU.mult)
            kks[jb] = kk

        def rra_g(jb):
            kk = work.tile([P, TOK], I32, name="kk", tag="kk", bufs=2)
            nc.vector.memset(kk[:, 0:1], 0)
            nc.gpsimd.tensor_scalar(
                out=kk[:], in0=niota[:], scalar1=fcol[:, jb : jb + 1], scalar2=0.0, op0=ALU.mult, op1=ALU.add
            )
            kks[jb] = kk
        def rrb(jb):
            nph = work.tile([P, TOK], F32, name="nph", tag="nph", bufs=2)
            nc.vector.scalar_tensor_tensor(out=nph[:], in0=niota[:], scalar=fcol[:, jb : jb + 1], in1=kks[jb][:], op0=ALU.mult, op1=ALU.subtract)
            nphs[jb] = nph
        mid4 = const.tile([P, 4], F32, name="mid4")
        nc.gpsimd.iota(mid4[:], pattern=[[512, 4]], base=255, channel_multiplier=0, allow_small_or_imprecise_dtypes=True)
        m8 = const.tile([P, 2, 4], I32, name="m8")
        q8 = const.tile([P, 2, 4], I32, name="q8")
        r8 = const.tile([P, 2, 4], F32, name="r8")
        s8 = const.tile([P, 2, 4], F32, name="s8")
        t8 = const.tile([P, 2, 4], F32, name="t8")
        b8 = const.tile([P, 2, 4], F32, name="b8")

        def ht(k):
            if k == 0:
                nc.vector.tensor_scalar(out=m8[:, 0, :], in0=mid4[:], scalar1=fcol[:, 2:3], scalar2=None, op0=ALU.mult)
                nc.vector.tensor_scalar(out=m8[:, 1, :], in0=mid4[:], scalar1=fcol[:, 2:3], scalar2=0.5, op0=ALU.mult, op1=ALU.add)
            elif k == 1:
                nc.vector.tensor_scalar(out=q8[:], in0=m8[:], scalar1=0.5, scalar2=None, op0=ALU.mult)
            elif k == 2:
                nc.vector.scalar_tensor_tensor(out=r8[:], in0=q8[:], scalar=-2.0, in1=m8[:], op0=ALU.mult, op1=ALU.add)
            elif k == 3:
                nc.vector.tensor_tensor(out=t8[:], in0=r8[:], in1=r8[:], op=ALU.mult)
            elif k == 4:
                nc.vector.tensor_scalar(out=s8[:], in0=t8[:], scalar1=-2.0, scalar2=1.0, op0=ALU.mult, op1=ALU.add)
            elif k == 5:
                nc.vector.scalar_tensor_tensor(out=b8[:], in0=m8[:], scalar=-math.pi, in1=s8[:], op0=ALU.mult, op1=ALU.mult)
                nc.vector.tensor_scalar(out=t8[:], in0=s8[:], scalar1=fcol[:, 2:3], scalar2=TWO_PI, op0=ALU.mult, op1=ALU.mult)
            else:
                nc.vector.scalar_tensor_tensor(
                    out=b8[:, 1, :], in0=s8[:, 1, :], scalar=0.5 * math.pi, in1=b8[:, 1, :], op0=ALU.mult, op1=ALU.add
                )

        def trig2(k):
            for c in range(4):
                cs = slice(256 * c, 256 * c + 256)
                nc.scalar.activation(
                    out=trig[:, 2, 1 - k, cs], in_=niota[:, cs], func=ACT.Sin, scale=t8[:, k, c : c + 1], bias=b8[:, k, c : c + 1]
                )

        def sin(jb):
            if jb == 3: nc.scalar.activation(out=trig[:, jb, 1, :], in_=niota[:], func=ACT.Sin, scale=ang3[:, 0:1])
            else: nc.scalar.activation(out=trig[:, jb, 1, :], in_=nphs[jb][:], func=ACT.Sin, scale=TWO_PI)
        def cos(jb):
            if jb == 3:
                nc.scalar.activation(out=trig[:, jb, 0, :], in_=niota[:], func=ACT.Sin, scale=ang3[:, 1:2], bias=halfpi[:])
                return
            ab = work.tile([P, TOK], F32, name="ab", tag="ab")
            nc.scalar.activation(out=ab[:], in_=nphs[jb][:], func=ACT.Abs)
            nc.scalar.activation(out=trig[:, jb, 0, :], in_=ab[:], func=ACT.Sin, scale=-TWO_PI, bias=halfpi[:])
        xcodes = const.tile([P, 2, 2, 512], U32, name="xcodes", align_bytes=64)
        xscl = const.tile([P, 2, 2, 512], U8, name="xscl", align_bytes=64)
        xg = {}; xws = {}; xts = {}
        def cast(h, a, on_vector=False):
            xw = work.tile([P, KDIM], BF16, name="xw", tag="xw", bufs=4)
            xws[(h, a)] = xw
            src = xbytes[h][:, a, :].bitcast(FP8)
            if on_vector:
                nc.vector.tensor_copy(out=xw[:], in_=src)
            else:
                nc.scalar.copy(out=xw[:], in_=src)
        def xt(h, i):
            xt = [ps_o.tile([P, 2, 256], F32, name="xt%d" % g, tag="ot") for g in range(2)]
            xts[(h, i)] = xt
            for aa in range(2):
                words = xws[(h, 2 * i + aa)][:].bitcast(F32)
                for g in range(2):
                    for u in range(2):
                        nc.tensor.transpose(xt[g][:, u, P * aa : P * aa + P], words[:, 256 * g + u : 256 * (g + 1) : 2], ident[:])
        def xsc(h, i, g):
            if h not in xg: xg[h] = work.tile([P, 2, 512, 4], BF16, name="xg", tag="xg", align_bytes=64)
            nc.vector.tensor_tensor(
                out=xg[h][:, g, 256 * i : 256 * i + 256, :].rearrange("p r (u e) -> p r u e", e=2),
                in0=xts[(h, i)][g][:].rearrange("p u r -> p (u r)").bitcast(BF16).rearrange("p (u r e) -> p r u e", u=2, e=2),
                in1=xs[:, g, :].rearrange("p (u e) -> p u e", e=2).unsqueeze(1).to_broadcast([P, 256, 2, 2]), op=ALU.mult)
        def xq(h):
            nc.vector.quantize_mx(out=xcodes[:, h, :, :].rearrange("p g r -> p (g r)").bitcast(FP8X4), scales=xscl[:, h, :, :].rearrange("p g r -> p (g r)"), in_=xg[h][:].rearrange("p g r t -> p (g r t)"))
        identb = const.tile([P, P], BF16, name="identb")
        nc.vector.tensor_copy(out=identb[:], in_=ident[:])
        wps = {}

        def wpe(o, jb, g, k):
            ps = ps_p.tile([P, 2, P, 4], BF16, name="wps", tag="acc%d" % k)
            wps[(o, jb, g)] = ps
            src = wraw[(o, jb, g)][:].rearrange("p t (j e) -> p e j t", e=2)
            for e in range(2):
                nc.tensor.matmul(out=ps[:, e, :, :], lhsT=identb[:], rhs=src[:, e, :, :], start=True, stop=True)

        def wout(o, jb, g):
            if (o, jb) not in wgs:
                wgs[(o, jb)] = work.tile([P, 2, 2, P, 4], BF16, name="wg", tag="wg", bufs=3, align_bytes=64)
            nc.vector.tensor_copy(out=wgs[(o, jb)][:, g, :, :, :], in_=wps[(o, jb, g)][:])

        wcodes = const.tile([P, 2, 4, 512], U32, name="wcodes", align_bytes=64)
        wscl = const.tile([P, 2, 4, 512], U8, name="wscl", align_bytes=64)
        wgs = {}
        def wil(o, jb, g, e="s"):
            if (o, jb) not in wgs:
                wgs[(o, jb)] = work.tile([P, 2, 2, P, 4], BF16, name="wg", tag="wg", bufs=3, align_bytes=64)
            wg = wgs[(o, jb)]
            src = wraw[(o, jb, g)][:].rearrange("p t (j e) -> p e j t", e=2)
            if e == "v": nc.vector.tensor_copy(out=wg[:, g, :, :, :], in_=src); return
            nc.scalar.copy(
                out=wg[:, g, :, :, :].rearrange("p e (c i) t -> p c t e i", i=4),
                in_=wraw[(o, jb, g)][:].rearrange("p t (c i e) -> p c t e i", i=4, e=2),
            )
        def wq(o, jb):
            nc.vector.quantize_mx(out=wcodes[:, o, jb, :].bitcast(FP8X4), scales=wscl[:, o, jb, :], in_=wgs[(o, jb)][:].rearrange("p g e j t -> p (g e j t)"))
        tabs = {}; banks = {}; prods = {}; otsd = {}
        gfac = const.tile([P, 4, 4], F32, name="gfac")
        def gf():
            nc.vector.tensor_copy(out=gfac[:, 0, :], in_=zcol[:])
            nc.vector.tensor_scalar(out=gfac[:, 1, :], in0=zcol[:], scalar1=-1.0, scalar2=None, op0=ALU.mult)
            nc.vector.reciprocal(out=gfac[:, 2, :], in_=zcol[:])
            nc.vector.tensor_scalar(out=gfac[:, 3, :], in0=gfac[:, 2, :], scalar1=-1.0, scalar2=None, op0=ALU.mult)
        tbs = {}

        def hold_tab(o, jb):
            tbs[(o, jb)] = work.tile([P, 2, 2, 512], F32, name="tb", tag="tb", bufs=2)
            nc.vector.memset(tbs[(o, jb)][:, 0, 0, 0:1], 0.0)

        def tab(o, jb):
            tb = tbs[(o, jb)]
            nc.gpsimd.tensor_tensor(
                out=tb[:].rearrange("p c h n -> p (c h) n"),
                in0=trig[:, jb, :, :].rearrange("p c (h n) -> p (c h) n", h=2),
                in1=sc0[:, 4 * o + jb, :].unsqueeze(1).to_broadcast([P, 4, 512]),
                op=ALU.mult,
            )
            for h in range(2):
                tabs[(o, jb, h)] = tb[:, :, h, :]

        def mx(o, jb, h, e):
            u = (o, jb, h)
            if u not in banks: banks[u] = {}
            acc = ps_p.tile([P, 512], F32, name="acc%d" % e, tag="acc%d" % e)
            banks[u][e] = acc
            for g in range(2):
                wc = slice(256 * g + P * e, 256 * g + P * e + P)
                nc.tensor.matmul_mx(out=acc[:], lhsT=wcodes[:, o, jb, wc].bitcast(FP8X4), lhsT_scale=wscl[:, o, jb, wc], rhs=xcodes[:, h, g, :].bitcast(FP8X4), rhs_scale=xscl[:, h, g, :], start=(g == 0), stop=(g == 1))
        def pr(u, c0=0, c1=512):
            o, jb, h = u
            tb = tabs[u]
            pe, po = banks[u][0], banks[u][1]
            if h == 0:
                gp, gn = 1.0, -1.0
            else:
                gp = gfac[:, 2 * o, jb : jb + 1]
                gn = gfac[:, 2 * o + 1, jb : jb + 1]
            if c0 == 0:
                prods[u] = [work.tile([P, 2, 512], F32, name="m%d" % e, tag="m%d" % e, bufs=3) for e in range(2)]
            me, mo = prods[u]
            cs = slice(c0, c1)
            nc.vector.scalar_tensor_tensor(
                out=me[:, :, cs], in0=tb[:, :, cs], scalar=gp, in1=pe[:, cs].unsqueeze(1).to_broadcast([P, 2, c1 - c0]), op0=ALU.mult, op1=ALU.mult
            )
            nc.vector.scalar_tensor_tensor(out=mo[:, 0, cs], in0=tb[:, 0, cs], scalar=gp, in1=po[:, cs], op0=ALU.mult, op1=ALU.mult)
            nc.vector.scalar_tensor_tensor(out=mo[:, 1, cs], in0=tb[:, 1, cs], scalar=gn, in1=po[:, cs], op0=ALU.mult, op1=ALU.mult)

        def tr(o, jb, h, q0, nq=2):
            u = (o, jb, h)
            me, mo = prods[u]
            ms = (me[:, 0, :], mo[:, 1, :], mo[:, 0, :], me[:, 1, :])
            ot = ps_o.tile([P, nq, 2, P], F32, name="ot", tag="ot")
            otsd[(u, q0)] = ot
            for e in range(2):
                for s in range(nq):
                    for z in range(2):
                        ts = slice(P * (q0 + s), P * (q0 + s) + P)
                        nc.tensor.matmul(
                            out=ot[:, s, e, :], lhsT=ms[2 * e + z][:, ts], rhs=ident[:], is_transpose=True, start=(z == 0), stop=(z == 1)
                        )

        def ev(o, jb, h, q0, nq=2, copy=nc.scalar.copy):
            ot = otsd[((o, jb, h), q0)]
            sg = work.tile([P, 2, 256], F32, name="stg", tag="stg", bufs=6)
            copy(out=sg[:, 0:nq, :].rearrange("p q (j e) -> p q j e", e=2), in_=ot[:].rearrange("p q e j -> p q j e"))
            t0 = 4 * h + q0
            nc.sync.dma_start(out=outs[o][:, t0 : t0 + nq, 256 * jb : 256 * jb + 256], in_=sg[:, 0:nq, :])

        units = [(o, jb, h) for jb in JB for o in range(2) for h in range(2)]
        n_units = len(units)

        prep = []
        for jb in JB[1:]:
            if jb == 2:
                waves = [(trig2, (1,)), (trig2, (0,))]
            else:
                waves = [(cos, (jb,)), (sin, (jb,))]
            if jb != JB[1]:
                prep += [(dbl, (jb,))]
            prep += [(wil, (0, jb, 0)), (wil, (0, jb, 1))] + waves
            prep += [(dbl, (4 + jb,)), (wil, (1, jb, 0)), (wil, (1, jb, 1))]
        n_head = 8
        n_spread = 10
        rest = prep[n_head:]

        def prep_s(items):
            for fn, a in items:
                fn(*a)

        rra(JB[1])
        freqs()
        gf()
        rads()
        cast(0, 0, True)
        ht(0)
        dbl_v(0, JB[0])
        ht(1)
        wil(0, JB[0], 0, "v")
        ht(2)
        dbl_v(1, JB[0])
        ht(3)
        wil(0, JB[0], 1, "v")
        ht(4)
        dbl_v(2, JB[0])
        ht(5)
        ht(6)
        rrb(JB[1])
        for a in range(1, 4):
            cast(0, a)
        rra_g(JB[2])
        dbl_g(4 + JB[0])
        dbl_g(JB[1])
        xt(0, 0)
        wpe(1, JB[0], 0, 0)
        xsc(0, 0, 0)
        xsc(0, 0, 1)
        xt(0, 1)
        wpe(1, JB[0], 1, 1)
        xsc(0, 1, 0)
        wout(1, JB[0], 0)
        xsc(0, 1, 1)
        wout(1, JB[0], 1)
        sin(JB[0])
        cast(1, 0)
        cast(1, 1)
        cos(JB[0])
        cast(1, 2)
        cast(1, 3)
        wq(0, JB[0])
        xq(0)
        hold_tab(0, JB[0])
        tab(0, JB[0])
        xt(1, 0)
        xt(1, 1)
        mx(*units[0], 0)
        mx(*units[0], 1)
        for i in range(2):
            xsc(1, i, 0)
            xsc(1, i, 1)
        xq(1)
        mx(*units[1], 0)
        mx(*units[1], 1)
        wq(1, JB[0])
        hold_tab(1, JB[0])
        tab(1, JB[0])
        prep_s(prep[:n_head])
        for n in range(n_units + 1):
            pair_ends = n % 2 == 1 and n + 3 < n_units
            if n < n_units - 1:
                pr(units[n])
                if pair_ends:
                    o, jb, h = units[n + 3]
                    wq(o, jb)
                    if n == 1:
                        rrb(JB[2])
                    hold_tab(o, jb)
            if n > 0:
                last = n == n_units
                parts = ((0, 2), (2, 1), (3, 1)) if last else ((0, 2), (2, 2))
                if n % 2 == 0:
                    for q0, nq in parts:
                        tr(*units[n - 1], q0, nq)
                for e in range(2):
                    if n + 1 < n_units:
                        mx(*units[n + 1], e)
                if n % 2 == 1:
                    for q0, nq in parts:
                        tr(*units[n - 1], q0, nq)
                for q0, nq in parts:
                    ev(*units[n - 1], q0, nq, nc.vector.tensor_copy if last and q0 == 2 else nc.scalar.copy)
            if n < n_spread:
                prep_s(rest[n * len(rest) // n_spread : (n + 1) * len(rest) // n_spread])
            if n == n_units - 1:
                for c0, c1 in ((0, 256), (256, 384), (384, 512)):
                    pr(units[n], c0, c1)
            if pair_ends:
                o, jb, h = units[n + 3]
                tab(o, jb)
